import numpy as np
import ml_dtypes

BF16 = ml_dtypes.bfloat16


def bf(x):
    return np.asarray(x, np.float32).astype(BF16)


def f32(x):
    return np.asarray(x, np.float32)


def f64(x):
    return np.asarray(x).astype(np.float64)


def striped(idx):
    return np.tile(idx.reshape(-1, 16).T, (8, 1))


C, S, N, H, DH, BS, NB = 512, 4096, 2048, 4, 128, 128, 16
EPS = 1e-5


def layer_norm(z, gain, bias):
    mu = z.mean(0, keepdims=True)
    zc = z - mu
    var = (zc * zc).mean(0, keepdims=True)
    return zc / np.sqrt(var + EPS) * gain + bias


def setup_inputs():
    return {
        "tok_emb": f32(np.random.standard_normal((C, S))),
        "pos_emb": f32(np.random.standard_normal((C, N))),
        "gain_e": f32(1.0 + 0.1 * np.random.standard_normal((C, 1))),
        "bias_e": f32(0.1 * np.random.standard_normal((C, 1))),
        "wq": bf(1.2 * np.random.standard_normal((C, C)) / np.sqrt(C)),
        "wk": bf(1.2 * np.random.standard_normal((C, C)) / np.sqrt(C)),
        "wv": bf(np.random.standard_normal((C, C)) / np.sqrt(C)),
        "wo": bf(2.0 * np.random.standard_normal((C, C)) / np.sqrt(C)),
        "gain1": f32(1.0 + 0.1 * np.random.standard_normal((C, 1))),
        "bias1": f32(0.1 * np.random.standard_normal((C, 1))),
        "offs": striped(np.random.permutation(np.tile(np.arange(S), 2))[:N]),
    }


def reference(tok_emb, pos_emb, gain_e, bias_e, wq, wk, wv, wo, gain1, bias1, offs):
    idx = offs[:16].T.reshape(-1)
    e = f64(tok_emb)[:, idx] + f64(pos_emb)
    x = layer_norm(e, f64(gain_e), f64(bias_e))
    q = (f64(wq).T @ x).reshape(H, DH, NB, BS)
    k = (f64(wk).T @ x).reshape(H, DH, NB, BS)
    v = (f64(wv).T @ x).reshape(H, DH, NB, BS)
    s = np.einsum("hdnq,hdnk->hnqk", q, k) / np.sqrt(DH)
    a = np.exp(s)
    a = a / a.sum(-1, keepdims=True)
    ctx = np.einsum("hnqk,hdnk->hdnq", a, v).reshape(C, N)
    y = x + f64(wo).T @ ctx
    return layer_norm(y, f64(gain1), f64(bias1))

@@ -1,0 +1,197 @@
+import math
+
+import concourse.mybir as mybir
+from concourse.masks import make_identity
+
+F32 = mybir.dt.float32
+BF16 = mybir.dt.bfloat16
+U16 = mybir.dt.uint16
+ALU = mybir.AluOpType
+ACT = mybir.ActivationFunctionType
+AX = mybir.AxisListType
+
+P = 128
+C = 512
+VOCAB = 4096
+N = 2048
+CB = C // P
+CHUNK = 512
+NCHUNK = N // CHUNK
+TB = CHUNK // P
+EPS = 1e-5
+SCALE = 1.0 / math.sqrt(P)
+
+FLOPS = 4 * 2 * C * C * N + 2 * 2 * P * P * P * CB * (N // P)
+
+
+def tile_proteintransformer_b_kernel(
+    tc, tok_emb, pos_emb, gain_e, bias_e, wq, wk, wv, wo, gain1, bias1, offs, out
+):
+    nc = tc.nc
+    with (
+        tc.tile_pool(name="held", bufs=1) as held,
+        tc.tile_pool(name="posp", bufs=NCHUNK) as posp,
+        tc.tile_pool(name="resp", bufs=NCHUNK) as resp,
+        tc.tile_pool(name="halfp", bufs=2) as halfp,
+        tc.tile_pool(name="statp", bufs=2) as statp,
+        tc.tile_pool(name="projp", bufs=2) as projp,
+        tc.tile_pool(name="attp", bufs=3) as attp,
+        tc.psum_pool(name="stat_ps", bufs=2) as stat_ps,
+        tc.psum_pool(name="acc_ps", bufs=2) as acc_ps,
+        tc.psum_pool(name="score_ps", bufs=2) as score_ps,
+        tc.psum_pool(name="att_ps", bufs=1) as att_ps,
+    ):
+        offsets = held.tile([P, N // 16], U16, name="offsets")
+        nc.sync.dma_start(offsets[:], offs)
+
+        pos_view = pos_emb.rearrange("(b p) n -> p b n", p=P)
+        out_view = out.rearrange("(b p) n -> p b n", p=P)
+        pos = [posp.tile([P, CB, CHUNK], F32, name="pos") for ch in range(NCHUNK)]
+        tok = [held.tile([P, VOCAB], F32, name="tok%d" % b) for b in range(CB)]
+        weights = {}
+        for name in ("wq", "wk", "wv", "wo"):
+            weights[name] = held.tile([P, CB, C], BF16, name=name + "_sb")
+
+        def load_pos(ch):
+            nc.sync.dma_start(pos[ch][:], pos_view[:, :, ch * CHUNK : (ch + 1) * CHUNK])
+
+        def load_weight(name, w):
+            nc.sync.dma_start(weights[name][:], w.rearrange("(kb p) m -> p kb m", p=P))
+
+        load_pos(0)
+        for b in range(CB):
+            nc.sync.dma_start(tok[b][:], tok_emb[b * P : (b + 1) * P, :])
+        load_weight("wq", wq)
+        load_weight("wk", wk)
+        load_weight("wv", wv)
+        load_pos(1)
+        load_weight("wo", wo)
+        load_pos(2)
+        load_pos(3)
+
+        per_channel = {}
+        with nc.allow_non_contiguous_dma(reason="four values to a partition"):
+            for name, vec in (("gain_e", gain_e), ("bias_e", bias_e), ("gain1", gain1), ("bias1", bias1)):
+                per_channel[name] = held.tile([P, CB], F32, name=name + "_sb")
+                nc.scalar.dma_start(per_channel[name][:], vec.rearrange("(b p) o -> p (b o)", p=P))
+
+        mean_w = held.tile([P, P], BF16, name="mean_w")
+        nc.vector.memset(mean_w[:], 1.0 / C)
+        ident = held.tile([P, P], BF16, name="ident")
+        make_identity(nc, ident[:])
+        eps = held.tile([P, 1], F32, name="eps")
+        nc.vector.memset(eps[:], EPS)
+
+        def mean_over_channels(half):
+            mean_ps = stat_ps.tile([P, CHUNK], F32, name="mean_ps")
+            for b in range(CB):
+                nc.tensor.matmul(mean_ps[:], mean_w[:], half[:, b, :], start=(b == 0), stop=(b == CB - 1))
+            return mean_ps
+
+        def normalise(res, gain):
+            z_bf = halfp.tile([P, CB, CHUNK], BF16, name="z_bf")
+            nc.gpsimd.tensor_scalar(z_bf[:], res[:], 1.0, 0.0, ALU.mult, ALU.add)
+            mean_ps = mean_over_channels(z_bf)
+            mean_bc = mean_ps[:].unsqueeze(1).to_broadcast([P, CB, CHUNK])
+            nc.vector.tensor_tensor(res[:], res[:], mean_bc, ALU.subtract)
+            sq_bf = halfp.tile([P, CB, CHUNK], BF16, name="sq_bf")
+            nc.scalar.activation(sq_bf[:], res[:], ACT.Square)
+            var_ps = mean_over_channels(sq_bf)
+            ln_var = statp.tile([P, CHUNK], F32, name="ln_var")
+            nc.scalar.activation(ln_var[:], var_ps[:], ACT.Ln, bias=eps[:])
+            rstd = statp.tile([P, CHUNK], F32, name="rstd")
+            nc.scalar.activation(rstd[:], ln_var[:], ACT.Exp, scale=-0.5)
+            for b in range(CB):
+                nc.vector.scalar_tensor_tensor(
+                    res[:, b, :], res[:, b, :], gain[:, b : b + 1], rstd[:], ALU.mult, ALU.mult
+                )
+
+        def project(w_sb, moving, dst):
+            for m in range(CB):
+                acc = acc_ps.tile([P, CHUNK], F32, name="acc")
+                for kb in range(CB):
+                    nc.tensor.matmul(
+                        acc[:], w_sb[:, kb, m * P : (m + 1) * P], moving[:, kb, :],
+                        start=(kb == 0), stop=(kb == CB - 1),
+                    )
+                nc.scalar.copy(dst[:, m, :], acc[:])
+
+        for ch in range(NCHUNK):
+            res = resp.tile([P, CB, CHUNK], F32, name="res")
+            piece = offsets[:, ch * (CHUNK // 16) : (ch + 1) * (CHUNK // 16)]
+            for b in range(CB):
+                nc.vector.tensor_tensor(res[:, b, :], tok[b][:].indirect(piece), pos[ch][:, b, :], ALU.add)
+
+            normalise(res, per_channel["gain_e"])
+            x_bf = projp.tile([P, CB, CHUNK], BF16, name="x_bf")
+            for b in range(CB):
+                nc.gpsimd.tensor_scalar(
+                    x_bf[:, b, :], res[:, b, :], 1.0, per_channel["bias_e"][:, b : b + 1], ALU.mult, ALU.add
+                )
+
+            q_bf = projp.tile([P, CB, CHUNK], BF16, name="q_bf")
+            k_bf = projp.tile([P, CB, CHUNK], BF16, name="k_bf")
+            project(weights["wq"], x_bf, q_bf)
+            project(weights["wk"], x_bf, k_bf)
+            v_tok = projp.tile([P, TB, C], BF16, name="v_tok")
+            for t in range(TB):
+                acc = acc_ps.tile([P, C], F32, name="acc")
+                for kb in range(CB):
+                    nc.tensor.matmul(
+                        acc[:], x_bf[:, kb, t * P : (t + 1) * P], weights["wv"][:, kb, :],
+                        start=(kb == 0), stop=(kb == CB - 1),
+                    )
+                nc.scalar.copy(v_tok[:, t, :], acc[:])
+
+            ctx_bf = projp.tile([P, CB, CHUNK], BF16, name="ctx_bf")
+            for t in range(TB):
+                blk = slice(t * P, (t + 1) * P)
+                s_ps = score_ps.tile([P, CB, P], F32, name="s_ps")
+                for h in range(CB):
+                    nc.tensor.matmul(s_ps[:, h, :], q_bf[:, h, blk], k_bf[:, h, blk], start=True, stop=True)
+                top = attp.tile([P, CB], F32, name="top")
+                nc.vector.reduce_max(top[:], s_ps[:], axis=AX.X)
+                shift = attp.tile([P, CB], F32, name="shift")
+                nc.vector.tensor_scalar_mul(shift[:], top[:], -SCALE)
+                expo = attp.tile([P, CB, P], F32, name="expo")
+                total = attp.tile([P, CB], F32, name="total")
+                for h in range(CB):
+                    nc.scalar.activation(
+                        expo[:, h, :], s_ps[:, h, :], ACT.Exp,
+                        bias=shift[:, h : h + 1], scale=SCALE, accum_out=total[:, h : h + 1],
+                    )
+                inv = attp.tile([P, CB], F32, name="inv")
+                nc.vector.reciprocal(inv[:], total[:])
+                a_bf = attp.tile([P, CB, P], BF16, name="a_bf")
+                nc.vector.tensor_tensor(
+                    a_bf[:], expo[:], inv[:].unsqueeze(2).to_broadcast([P, CB, P]), ALU.mult
+                )
+                aT_ps = att_ps.tile([P, CB, P], BF16, name="aT_ps")
+                for h in range(CB):
+                    nc.tensor.transpose(aT_ps[:, h, :], a_bf[:, h, :], ident[:])
+                aT_bf = attp.tile([P, CB, P], BF16, name="aT_bf")
+                nc.vector.tensor_copy(aT_bf[:], aT_ps[:])
+                ctx_ps = att_ps.tile([P, CB, P], F32, name="ctx_ps")
+                for h in range(CB):
+                    nc.tensor.matmul(
+                        ctx_ps[:, h, :], v_tok[:, t, h * P : (h + 1) * P], aT_bf[:, h, :], start=True, stop=True
+                    )
+                nc.scalar.copy(ctx_bf[:, :, blk], ctx_ps[:])
+
+            for m in range(CB):
+                acc = acc_ps.tile([P, CHUNK], F32, name="acc")
+                for kb in range(CB):
+                    nc.tensor.matmul(
+                        acc[:], weights["wo"][:, kb, m * P : (m + 1) * P], ctx_bf[:, kb, :],
+                        start=(kb == 0), stop=(kb == CB - 1),
+                    )
+                nc.vector.scalar_tensor_tensor(
+                    res[:, m, :], acc[:], per_channel["bias_e"][:, m : m + 1], res[:, m, :], ALU.add, ALU.add
+                )
+
+            normalise(res, per_channel["gain1"])
+            for b in range(CB):
+                nc.gpsimd.tensor_scalar(
+                    res[:, b, :], res[:, b, :], 1.0, per_channel["bias1"][:, b : b + 1], ALU.mult, ALU.add
+                )
+            nc.sync.dma_start(out_view[:, :, ch * CHUNK : (ch + 1) * CHUNK], res[:])

@@ -15,13 +15,15 @@ C = 512
 VOCAB = 4096
 N = 2048
 CB = C // P
+NBLK = N // P
 CHUNK = 512
 NCHUNK = N // CHUNK
 TB = CHUNK // P
+PER_STEP = 3 * CB // TB
 EPS = 1e-5
 SCALE = 1.0 / math.sqrt(P)
 
-FLOPS = 4 * 2 * C * C * N + 2 * 2 * P * P * P * CB * (N // P)
+FLOPS = 4 * 2 * C * C * N + 2 * 2 * P * P * P * CB * NBLK
 
 
 def tile_proteintransformer_b_kernel(
@@ -30,168 +32,214 @@ def tile_proteintransformer_b_kernel(
     nc = tc.nc
     with (
         tc.tile_pool(name="held", bufs=1) as held,
-        tc.tile_pool(name="posp", bufs=NCHUNK) as posp,
-        tc.tile_pool(name="resp", bufs=NCHUNK) as resp,
-        tc.tile_pool(name="halfp", bufs=2) as halfp,
-        tc.tile_pool(name="statp", bufs=2) as statp,
-        tc.tile_pool(name="projp", bufs=2) as projp,
-        tc.tile_pool(name="attp", bufs=3) as attp,
-        tc.psum_pool(name="stat_ps", bufs=2) as stat_ps,
-        tc.psum_pool(name="acc_ps", bufs=2) as acc_ps,
-        tc.psum_pool(name="score_ps", bufs=2) as score_ps,
-        tc.psum_pool(name="att_ps", bufs=1) as att_ps,
+        tc.tile_pool(name="chunkp", bufs=2) as chunkp,
+        tc.tile_pool(name="resp", bufs=14) as resp,
+        tc.tile_pool(name="blockp", bufs=3) as blockp,
+        tc.psum_pool(name="flip_ps", bufs=1) as flip_ps,
+        tc.psum_pool(name="qkv_ps", bufs=2) as qkv_ps,
+        tc.psum_pool(name="score_ps", bufs=1) as score_ps,
+        tc.psum_pool(name="emb_ps", bufs=2) as emb_ps,
     ):
         offsets = held.tile([P, N // 16], U16, name="offsets")
         nc.sync.dma_start(offsets[:], offs)
 
         pos_view = pos_emb.rearrange("(b p) n -> p b n", p=P)
         out_view = out.rearrange("(b p) n -> p b n", p=P)
-        pos = [posp.tile([P, CB, CHUNK], F32, name="pos") for ch in range(NCHUNK)]
         tok = [held.tile([P, VOCAB], F32, name="tok%d" % b) for b in range(CB)]
         weights = {}
         for name in ("wq", "wk", "wv", "wo"):
             weights[name] = held.tile([P, CB, C], BF16, name=name + "_sb")
 
         def load_pos(ch):
-            nc.sync.dma_start(pos[ch][:], pos_view[:, :, ch * CHUNK : (ch + 1) * CHUNK])
+            pos = chunkp.tile([P, CB, CHUNK], F32, name="pos")
+            nc.sync.dma_start(pos[:], pos_view[:, :, ch * CHUNK : (ch + 1) * CHUNK])
+            return pos
 
         def load_weight(name, w):
             nc.sync.dma_start(weights[name][:], w.rearrange("(kb p) m -> p kb m", p=P))
 
-        load_pos(0)
+        pos_of = {0: load_pos(0)}
         for b in range(CB):
             nc.sync.dma_start(tok[b][:], tok_emb[b * P : (b + 1) * P, :])
         load_weight("wq", wq)
         load_weight("wk", wk)
         load_weight("wv", wv)
-        load_pos(1)
+        pos_of[1] = load_pos(1)
         load_weight("wo", wo)
-        load_pos(2)
-        load_pos(3)
 
         per_channel = {}
         with nc.allow_non_contiguous_dma(reason="four values to a partition"):
             for name, vec in (("gain_e", gain_e), ("bias_e", bias_e), ("gain1", gain1), ("bias1", bias1)):
                 per_channel[name] = held.tile([P, CB], F32, name=name + "_sb")
                 nc.scalar.dma_start(per_channel[name][:], vec.rearrange("(b p) o -> p (b o)", p=P))
+        gain_row = held.tile([P, C], F32, name="gain_row")
+        nc.scalar.dma_start(gain_row[:], gain_e.rearrange("c o -> (o c)").partition_broadcast(P))
+        bias_row = held.tile([P, C], F32, name="bias_row")
+        nc.scalar.dma_start(bias_row[:], bias_e.rearrange("c o -> (o c)").partition_broadcast(P))
 
-        mean_w = held.tile([P, P], BF16, name="mean_w")
-        nc.vector.memset(mean_w[:], 1.0 / C)
-        ident = held.tile([P, P], BF16, name="ident")
-        make_identity(nc, ident[:])
-        eps = held.tile([P, 1], F32, name="eps")
-        nc.vector.memset(eps[:], EPS)
+        ident_f32 = held.tile([P, P], F32, name="ident_f32")
+        make_identity(nc, ident_f32[:])
+        ident_bf = held.tile([P, P], BF16, name="ident_bf")
+        make_identity(nc, ident_bf[:])
+        minus_half = held.tile([P, 1], F32, name="minus_half")
+        nc.vector.memset(minus_half[:], -0.5)
 
-        def mean_over_channels(half):
-            mean_ps = stat_ps.tile([P, CHUNK], F32, name="mean_ps")
-            for b in range(CB):
-                nc.tensor.matmul(mean_ps[:], mean_w[:], half[:, b, :], start=(b == 0), stop=(b == CB - 1))
-            return mean_ps
+        emb_of = {}
+        x_of = {}
+        qkv_of = {}
+        flipped_of = {}
+        moments_of = {}
+        res_of = {}
+        a_of = {}
+        ctx_of = {}
 
-        def normalise(res, gain):
-            z_bf = halfp.tile([P, CB, CHUNK], BF16, name="z_bf")
-            nc.gpsimd.tensor_scalar(z_bf[:], res[:], 1.0, 0.0, ALU.mult, ALU.add)
-            mean_ps = mean_over_channels(z_bf)
-            mean_bc = mean_ps[:].unsqueeze(1).to_broadcast([P, CB, CHUNK])
-            nc.vector.tensor_tensor(res[:], res[:], mean_bc, ALU.subtract)
-            sq_bf = halfp.tile([P, CB, CHUNK], BF16, name="sq_bf")
-            nc.scalar.activation(sq_bf[:], res[:], ACT.Square)
-            var_ps = mean_over_channels(sq_bf)
-            ln_var = statp.tile([P, CHUNK], F32, name="ln_var")
-            nc.scalar.activation(ln_var[:], var_ps[:], ACT.Ln, bias=eps[:])
-            rstd = statp.tile([P, CHUNK], F32, name="rstd")
-            nc.scalar.activation(rstd[:], ln_var[:], ACT.Exp, scale=-0.5)
-            for b in range(CB):
-                nc.vector.scalar_tensor_tensor(
-                    res[:, b, :], res[:, b, :], gain[:, b : b + 1], rstd[:], ALU.mult, ALU.mult
-                )
-
-        def project(w_sb, moving, dst):
-            for m in range(CB):
-                acc = acc_ps.tile([P, CHUNK], F32, name="acc")
-                for kb in range(CB):
-                    nc.tensor.matmul(
-                        acc[:], w_sb[:, kb, m * P : (m + 1) * P], moving[:, kb, :],
-                        start=(kb == 0), stop=(kb == CB - 1),
-                    )
-                nc.scalar.copy(dst[:, m, :], acc[:])
-
-        for ch in range(NCHUNK):
-            res = resp.tile([P, CB, CHUNK], F32, name="res")
+        def lookup(ch):
+            emb = chunkp.tile([P, CB, CHUNK], F32, name="emb")
             piece = offsets[:, ch * (CHUNK // 16) : (ch + 1) * (CHUNK // 16)]
             for b in range(CB):
-                nc.vector.tensor_tensor(res[:, b, :], tok[b][:].indirect(piece), pos[ch][:, b, :], ALU.add)
+                nc.vector.tensor_tensor(emb[:, b, :], tok[b][:].indirect(piece), pos_of[ch][:, b, :], ALU.add)
+            emb_of[ch] = emb
+            if ch + 2 < NCHUNK:
+                pos_of[ch + 2] = load_pos(ch + 2)
 
-            normalise(res, per_channel["gain_e"])
-            x_bf = projp.tile([P, CB, CHUNK], BF16, name="x_bf")
+        def moments(j, z):
+            stats = blockp.tile([P, 6], F32, name="stats")
+            nc.vector.bn_stats(stats[:], z)
+            mean_var = blockp.tile([P, 2], F32, name="mean_var")
+            nc.vector.bn_aggr(mean_var[:], stats[:])
+            var_eps = blockp.tile([P, 1], F32, name="var_eps")
+            nc.vector.tensor_scalar_add(var_eps[:], mean_var[:, 1:2], EPS)
+            rstd = blockp.tile([P, 1], F32, name="rstd")
+            nc.gpsimd.tensor_tensor(rstd[:], var_eps[:], minus_half[:], ALU.pow)
+            moments_of[j] = (mean_var, rstd)
+
+        def normalise_and_flip(j, z):
+            mean_var, rstd = moments_of[j]
+            zn = blockp.tile([P, C], F32, name="zn")
+            nc.vector.tensor_scalar(zn[:], z, mean_var[:, 0:1], rstd[:], ALU.subtract, ALU.mult)
+            zn_ps = flip_ps.tile([P, CB, P], F32, name="zn_ps")
             for b in range(CB):
-                nc.gpsimd.tensor_scalar(
-                    x_bf[:, b, :], res[:, b, :], 1.0, per_channel["bias_e"][:, b : b + 1], ALU.mult, ALU.add
-                )
+                nc.tensor.transpose(zn_ps[:, b, :], zn[:, b * P : (b + 1) * P], ident_f32[:])
+            return zn, zn_ps
 
-            q_bf = projp.tile([P, CB, CHUNK], BF16, name="q_bf")
-            k_bf = projp.tile([P, CB, CHUNK], BF16, name="k_bf")
-            project(weights["wq"], x_bf, q_bf)
-            project(weights["wk"], x_bf, k_bf)
-            v_tok = projp.tile([P, TB, C], BF16, name="v_tok")
-            for t in range(TB):
-                acc = acc_ps.tile([P, C], F32, name="acc")
-                for kb in range(CB):
+        def embed_norm_1(j):
+            ch, t = divmod(j, TB)
+            if t == 0:
+                lookup(ch)
+            eT_ps = emb_ps.tile([P, C], F32, name="eT_ps")
+            for b in range(CB):
+                nc.tensor.transpose(eT_ps[:, b * P : (b + 1) * P], emb_of[ch][:, b, t * P : (t + 1) * P], ident_f32[:])
+            flipped_of[j] = eT_ps
+            moments(j, eT_ps[:])
+
+        def embed_norm_2(j):
+            ch, t = divmod(j, TB)
+            if t == 0:
+                x_of[ch] = chunkp.tile([P, CB, CHUNK], BF16, name="x_bf")
+            zn, zn_ps = normalise_and_flip(j, flipped_of[j][:])
+            for b in range(CB):
+                nc.scalar.activation(
+                    x_of[ch][:, b, t * P : (t + 1) * P], zn_ps[:, b, :], ACT.Identity,
+                    bias=per_channel["bias_e"][:, b : b + 1], scale=per_channel["gain_e"][:, b : b + 1],
+                )
+            res = resp.tile([P, C], F32, name="res")
+            nc.gpsimd.tensor_tensor(res[:], zn[:], gain_row[:], ALU.mult)
+            nc.gpsimd.tensor_tensor(res[:], res[:], bias_row[:], ALU.add)
+            res_of[j] = res
+
+        def project(ch, g):
+            if g == 0:
+                qkv_of[ch] = (
+                    chunkp.tile([P, CB, CHUNK], BF16, name="q_bf"),
+                    chunkp.tile([P, CB, CHUNK], BF16, name="k_bf"),
+                    chunkp.tile([P, TB, C], BF16, name="v_tok"),
+                )
+            x_bf = x_of[ch]
+            which, i = divmod(g, CB)
+            acc = qkv_ps.tile([P, CHUNK], F32, name="acc")
+            for kb in range(CB):
+                if which < 2:
+                    w_sb = weights[("wq", "wk")[which]]
                     nc.tensor.matmul(
-                        acc[:], x_bf[:, kb, t * P : (t + 1) * P], weights["wv"][:, kb, :],
+                        acc[:], w_sb[:, kb, i * P : (i + 1) * P], x_bf[:, kb, :], start=(kb == 0), stop=(kb == CB - 1)
+                    )
+                else:
+                    nc.tensor.matmul(
+                        acc[:], x_bf[:, kb, i * P : (i + 1) * P], weights["wv"][:, kb, :],
                         start=(kb == 0), stop=(kb == CB - 1),
                     )
-                nc.scalar.copy(v_tok[:, t, :], acc[:])
+            nc.scalar.copy(qkv_of[ch][which][:, i, :], acc[:])
 
-            ctx_bf = projp.tile([P, CB, CHUNK], BF16, name="ctx_bf")
-            for t in range(TB):
-                blk = slice(t * P, (t + 1) * P)
-                s_ps = score_ps.tile([P, CB, P], F32, name="s_ps")
-                for h in range(CB):
-                    nc.tensor.matmul(s_ps[:, h, :], q_bf[:, h, blk], k_bf[:, h, blk], start=True, stop=True)
-                top = attp.tile([P, CB], F32, name="top")
-                nc.vector.reduce_max(top[:], s_ps[:], axis=AX.X)
-                shift = attp.tile([P, CB], F32, name="shift")
-                nc.vector.tensor_scalar_mul(shift[:], top[:], -SCALE)
-                expo = attp.tile([P, CB, P], F32, name="expo")
-                total = attp.tile([P, CB], F32, name="total")
-                for h in range(CB):
-                    nc.scalar.activation(
-                        expo[:, h, :], s_ps[:, h, :], ACT.Exp,
-                        bias=shift[:, h : h + 1], scale=SCALE, accum_out=total[:, h : h + 1],
-                    )
-                inv = attp.tile([P, CB], F32, name="inv")
-                nc.vector.reciprocal(inv[:], total[:])
-                a_bf = attp.tile([P, CB, P], BF16, name="a_bf")
-                nc.vector.tensor_tensor(
-                    a_bf[:], expo[:], inv[:].unsqueeze(2).to_broadcast([P, CB, P]), ALU.mult
+        def scores(j):
+            ch, t = divmod(j, TB)
+            blk = slice(t * P, (t + 1) * P)
+            q_bf, k_bf = qkv_of[ch][0], qkv_of[ch][1]
+            s_ps = score_ps.tile([P, CB, P], F32, name="s_ps")
+            for h in range(CB):
+                nc.tensor.matmul(s_ps[:, h, :], q_bf[:, h, blk], k_bf[:, h, blk], start=True, stop=True)
+            top = blockp.tile([P, CB], F32, name="top")
+            nc.vector.reduce_max(top[:], s_ps[:], axis=AX.X)
+            neg_top = blockp.tile([P, CB], F32, name="neg_top")
+            nc.vector.tensor_scalar_mul(neg_top[:], top[:], -SCALE)
+            expo = blockp.tile([P, CB, P], F32, name="expo")
+            total = blockp.tile([P, CB], F32, name="total")
+            for h in range(CB):
+                nc.scalar.activation(
+                    expo[:, h, :], s_ps[:, h, :], ACT.Exp,
+                    bias=neg_top[:, h : h + 1], scale=SCALE, accum_out=total[:, h : h + 1],
                 )
-                aT_ps = att_ps.tile([P, CB, P], BF16, name="aT_ps")
-                for h in range(CB):
-                    nc.tensor.transpose(aT_ps[:, h, :], a_bf[:, h, :], ident[:])
-                aT_bf = attp.tile([P, CB, P], BF16, name="aT_bf")
-                nc.vector.tensor_copy(aT_bf[:], aT_ps[:])
-                ctx_ps = att_ps.tile([P, CB, P], F32, name="ctx_ps")
-                for h in range(CB):
-                    nc.tensor.matmul(
-                        ctx_ps[:, h, :], v_tok[:, t, h * P : (h + 1) * P], aT_bf[:, h, :], start=True, stop=True
-                    )
-                nc.scalar.copy(ctx_bf[:, :, blk], ctx_ps[:])
+            inv = blockp.tile([P, CB], F32, name="inv")
+            nc.vector.reciprocal(inv[:], total[:])
+            a_bf = blockp.tile([P, CB, P], BF16, name="a_bf")
+            nc.vector.tensor_tensor(a_bf[:], expo[:], inv[:].unsqueeze(2).to_broadcast([P, CB, P]), ALU.mult)
+            a_of[j] = a_bf
 
-            for m in range(CB):
-                acc = acc_ps.tile([P, CHUNK], F32, name="acc")
-                for kb in range(CB):
-                    nc.tensor.matmul(
-                        acc[:], weights["wo"][:, kb, m * P : (m + 1) * P], ctx_bf[:, kb, :],
-                        start=(kb == 0), stop=(kb == CB - 1),
-                    )
-                nc.vector.scalar_tensor_tensor(
-                    res[:, m, :], acc[:], per_channel["bias_e"][:, m : m + 1], res[:, m, :], ALU.add, ALU.add
+        def context(j):
+            ch, t = divmod(j, TB)
+            v_tok = qkv_of[ch][2]
+            a_bf = a_of[j]
+            flip_ctx = flip_ps.tile([P, 2, CB, P], BF16, name="flip_ctx")
+            for h in range(CB):
+                nc.tensor.transpose(flip_ctx[:, 0, h, :], a_bf[:, h, :], ident_bf[:])
+            aT_bf = blockp.tile([P, CB, P], BF16, name="aT_bf")
+            nc.scalar.copy(aT_bf[:], flip_ctx[:, 0, :, :])
+            for h in range(CB):
+                nc.tensor.matmul(
+                    flip_ctx[:, 1, h, :], v_tok[:, t, h * P : (h + 1) * P], aT_bf[:, h, :], start=True, stop=True
                 )
+            ctx_bf = blockp.tile([P, CB, P], BF16, name="ctx_bf")
+            nc.scalar.copy(ctx_bf[:], flip_ctx[:, 1, :, :])
+            ctx_of[j] = ctx_bf
 
-            normalise(res, per_channel["gain1"])
+        def residual(j):
+            ctx_bf = ctx_of[j]
+            yT_ps = flip_ps.tile([P, C], F32, name="yT_ps")
+            for kb in range(CB):
+                nc.tensor.matmul(yT_ps[:], ctx_bf[:, kb, :], weights["wo"][:, kb, :], start=(kb == 0), stop=(kb == CB - 1))
+            nc.vector.tensor_tensor(res_of[j][:], yT_ps[:], res_of[j][:], ALU.add)
+            moments(j, res_of[j][:])
+
+        def final_norm(j):
+            zn, zn_ps = normalise_and_flip(j, res_of[j][:])
+            done = blockp.tile([P, CB, P], F32, name="done")
             for b in range(CB):
-                nc.gpsimd.tensor_scalar(
-                    res[:, b, :], res[:, b, :], 1.0, per_channel["bias1"][:, b : b + 1], ALU.mult, ALU.add
+                nc.scalar.activation(
+                    done[:, b, :], zn_ps[:, b, :], ACT.Identity,
+                    bias=per_channel["bias1"][:, b : b + 1], scale=per_channel["gain1"][:, b : b + 1],
                 )
-            nc.sync.dma_start(out_view[:, :, ch * CHUNK : (ch + 1) * CHUNK], res[:])
+            nc.sync.dma_start(out_view[:, :, j * P : (j + 1) * P], done[:])
+
+        def if_block(stage, j):
+            if 0 <= j < NBLK:
+                stage(j)
+
+        for s in range(-5, NBLK + 7):
+            if_block(embed_norm_2, s + 4)
+            if_block(final_norm, s - 6)
+            if_block(context, s - 4)
+            if_block(residual, s - 5)
+            if_block(embed_norm_1, s + 5)
+            if_block(scores, s - 3)
+            if 0 <= s < NBLK:
+                for g in range((s % TB) * PER_STEP, (s % TB + 1) * PER_STEP):
+                    project(s // TB, g)

@@ -37,8 +37,7 @@ def tile_proteintransformer_b_kernel(
         tc.tile_pool(name="blockp", bufs=3) as blockp,
         tc.psum_pool(name="flip_ps", bufs=1) as flip_ps,
         tc.psum_pool(name="qkv_ps", bufs=2) as qkv_ps,
-        tc.psum_pool(name="score_ps", bufs=1) as score_ps,
-        tc.psum_pool(name="emb_ps", bufs=2) as emb_ps,
+        tc.psum_pool(name="score_ps", bufs=2) as score_ps,
     ):
         offsets = held.tile([P, N // 16], U16, name="offsets")
         nc.sync.dma_start(offsets[:], offs)
@@ -84,23 +83,24 @@ def tile_proteintransformer_b_kernel(
         minus_half = held.tile([P, 1], F32, name="minus_half")
         nc.vector.memset(minus_half[:], -0.5)
 
-        emb_of = {}
         x_of = {}
         qkv_of = {}
-        flipped_of = {}
         moments_of = {}
         res_of = {}
         a_of = {}
         ctx_of = {}
 
-        def lookup(ch):
-            emb = chunkp.tile([P, CB, CHUNK], F32, name="emb")
-            piece = offsets[:, ch * (CHUNK // 16) : (ch + 1) * (CHUNK // 16)]
+        def lookup(j):
+            ch, t = divmod(j, TB)
+            emb = blockp.tile([P, CB, P], F32, name="emb")
+            piece = offsets[:, j * (P // 16) : (j + 1) * (P // 16)]
             for b in range(CB):
-                nc.vector.tensor_tensor(emb[:, b, :], tok[b][:].indirect(piece), pos_of[ch][:, b, :], ALU.add)
-            emb_of[ch] = emb
-            if ch + 2 < NCHUNK:
+                nc.vector.tensor_tensor(
+                    emb[:, b, :], tok[b][:].indirect(piece), pos_of[ch][:, b, t * P : (t + 1) * P], ALU.add
+                )
+            if t == TB - 1 and ch + 2 < NCHUNK:
                 pos_of[ch + 2] = load_pos(ch + 2)
+            return emb
 
         def moments(j, z):
             stats = blockp.tile([P, 6], F32, name="stats")
@@ -113,39 +113,30 @@ def tile_proteintransformer_b_kernel(
             nc.gpsimd.tensor_tensor(rstd[:], var_eps[:], minus_half[:], ALU.pow)
             moments_of[j] = (mean_var, rstd)
 
-        def normalise_and_flip(j, z):
-            mean_var, rstd = moments_of[j]
-            zn = blockp.tile([P, C], F32, name="zn")
-            nc.vector.tensor_scalar(zn[:], z, mean_var[:, 0:1], rstd[:], ALU.subtract, ALU.mult)
-            zn_ps = flip_ps.tile([P, CB, P], F32, name="zn_ps")
+        def flip_back(z):
+            back_ps = flip_ps.tile([P, CB, P], F32, name="back_ps")
             for b in range(CB):
-                nc.tensor.transpose(zn_ps[:, b, :], zn[:, b * P : (b + 1) * P], ident_f32[:])
-            return zn, zn_ps
+                nc.tensor.transpose(back_ps[:, b, :], z[:, b * P : (b + 1) * P], ident_f32[:])
+            return back_ps
 
         def embed_norm_1(j):
-            ch, t = divmod(j, TB)
-            if t == 0:
-                lookup(ch)
-            eT_ps = emb_ps.tile([P, C], F32, name="eT_ps")
+            emb = lookup(j)
+            eT_ps = flip_ps.tile([P, C], F32, name="eT_ps")
             for b in range(CB):
-                nc.tensor.transpose(eT_ps[:, b * P : (b + 1) * P], emb_of[ch][:, b, t * P : (t + 1) * P], ident_f32[:])
-            flipped_of[j] = eT_ps
+                nc.tensor.transpose(eT_ps[:, b * P : (b + 1) * P], emb[:, b, :], ident_f32[:])
             moments(j, eT_ps[:])
+            res = resp.tile([P, C], F32, name="res")
+            nc.vector.scalar_tensor_tensor(res[:], eT_ps[:], moments_of[j][0][:, 0:1], gain_row[:], ALU.subtract, ALU.mult)
+            res_of[j] = res
 
         def embed_norm_2(j):
             ch, t = divmod(j, TB)
             if t == 0:
                 x_of[ch] = chunkp.tile([P, CB, CHUNK], BF16, name="x_bf")
-            zn, zn_ps = normalise_and_flip(j, flipped_of[j][:])
-            for b in range(CB):
-                nc.scalar.activation(
-                    x_of[ch][:, b, t * P : (t + 1) * P], zn_ps[:, b, :], ACT.Identity,
-                    bias=per_channel["bias_e"][:, b : b + 1], scale=per_channel["gain_e"][:, b : b + 1],
-                )
-            res = resp.tile([P, C], F32, name="res")
-            nc.gpsimd.tensor_tensor(res[:], zn[:], gain_row[:], ALU.mult)
-            nc.gpsimd.tensor_tensor(res[:], res[:], bias_row[:], ALU.add)
-            res_of[j] = res
+            res = res_of[j]
+            nc.vector.scalar_tensor_tensor(res[:], res[:], moments_of[j][1][:], bias_row[:], ALU.mult, ALU.add)
+            x_ps = flip_back(res)
+            nc.scalar.copy(x_of[ch][:, :, t * P : (t + 1) * P], x_ps[:])
 
         def project(ch, g):
             if g == 0:
@@ -168,7 +159,7 @@ def tile_proteintransformer_b_kernel(
                         acc[:], x_bf[:, kb, i * P : (i + 1) * P], weights["wv"][:, kb, :],
                         start=(kb == 0), stop=(kb == CB - 1),
                     )
-            nc.scalar.copy(qkv_of[ch][which][:, i, :], acc[:])
+            nc.scalar.mul(qkv_of[ch][which][:, i, :], acc[:], SCALE if which == 0 else 1.0)
 
         def scores(j):
             ch, t = divmod(j, TB)
@@ -177,21 +168,20 @@ def tile_proteintransformer_b_kernel(
             s_ps = score_ps.tile([P, CB, P], F32, name="s_ps")
             for h in range(CB):
                 nc.tensor.matmul(s_ps[:, h, :], q_bf[:, h, blk], k_bf[:, h, blk], start=True, stop=True)
-            top = blockp.tile([P, CB], F32, name="top")
-            nc.vector.reduce_max(top[:], s_ps[:], axis=AX.X)
             neg_top = blockp.tile([P, CB], F32, name="neg_top")
-            nc.vector.tensor_scalar_mul(neg_top[:], top[:], -SCALE)
+            nc.vector.reduce_max(neg_top[:], s_ps[:], axis=AX.X, negate=True)
             expo = blockp.tile([P, CB, P], F32, name="expo")
             total = blockp.tile([P, CB], F32, name="total")
             for h in range(CB):
                 nc.scalar.activation(
                     expo[:, h, :], s_ps[:, h, :], ACT.Exp,
-                    bias=neg_top[:, h : h + 1], scale=SCALE, accum_out=total[:, h : h + 1],
+                    bias=neg_top[:, h : h + 1], accum_out=total[:, h : h + 1],
                 )
             inv = blockp.tile([P, CB], F32, name="inv")
             nc.vector.reciprocal(inv[:], total[:])
             a_bf = blockp.tile([P, CB, P], BF16, name="a_bf")
-            nc.vector.tensor_tensor(a_bf[:], expo[:], inv[:].unsqueeze(2).to_broadcast([P, CB, P]), ALU.mult)
+            for h in range(CB):
+                nc.scalar.activation(a_bf[:, h, :], expo[:, h, :], ACT.Copy, scale=inv[:, h : h + 1])
             a_of[j] = a_bf
 
         def context(j):
@@ -220,7 +210,10 @@ def tile_proteintransformer_b_kernel(
             moments(j, res_of[j][:])
 
         def final_norm(j):
-            zn, zn_ps = normalise_and_flip(j, res_of[j][:])
+            mean_var, rstd = moments_of[j]
+            zn = blockp.tile([P, C], F32, name="zn")
+            nc.vector.tensor_scalar(zn[:], res_of[j][:], mean_var[:, 0:1], rstd[:], ALU.subtract, ALU.mult)
+            zn_ps = flip_back(zn)
             done = blockp.tile([P, CB, P], F32, name="done")
             for b in range(CB):
                 nc.scalar.activation(

@@ -19,9 +19,17 @@ NBLK = N // P
 CHUNK = 512
 NCHUNK = N // CHUNK
 TB = CHUNK // P
-PER_STEP = 3 * CB // TB
 EPS = 1e-5
 SCALE = 1.0 / math.sqrt(P)
+
+PER_STEP = 3 * CB // TB
+NORM_AHEAD = TB
+FLIP_AHEAD = NORM_AHEAD + 1
+SCORES_BEHIND = 2 * CB // PER_STEP + 1
+CONTEXT_BEHIND = SCORES_BEHIND + 1
+RESIDUAL_BEHIND = CONTEXT_BEHIND + 1
+OUT_BEHIND = RESIDUAL_BEHIND + 1
+RES_BUFS = FLIP_AHEAD + OUT_BEHIND + 1 + 2
 
 FLOPS = 4 * 2 * C * C * N + 2 * 2 * P * P * P * CB * NBLK
 
@@ -33,7 +41,7 @@ def tile_proteintransformer_b_kernel(
     with (
         tc.tile_pool(name="held", bufs=1) as held,
         tc.tile_pool(name="chunkp", bufs=2) as chunkp,
-        tc.tile_pool(name="resp", bufs=14) as resp,
+        tc.tile_pool(name="resp", bufs=RES_BUFS) as resp,
         tc.tile_pool(name="blockp", bufs=3) as blockp,
         tc.psum_pool(name="flip_ps", bufs=1) as flip_ps,
         tc.psum_pool(name="qkv_ps", bufs=2) as qkv_ps,
@@ -44,37 +52,39 @@ def tile_proteintransformer_b_kernel(
 
         pos_view = pos_emb.rearrange("(b p) n -> p b n", p=P)
         out_view = out.rearrange("(b p) n -> p b n", p=P)
-        tok = [held.tile([P, VOCAB], F32, name="tok%d" % b) for b in range(CB)]
-        weights = {}
-        for name in ("wq", "wk", "wv", "wo"):
-            weights[name] = held.tile([P, CB, C], BF16, name=name + "_sb")
 
         def load_pos(ch):
             pos = chunkp.tile([P, CB, CHUNK], F32, name="pos")
             nc.sync.dma_start(pos[:], pos_view[:, :, ch * CHUNK : (ch + 1) * CHUNK])
             return pos
 
-        def load_weight(name, w):
-            nc.sync.dma_start(weights[name][:], w.rearrange("(kb p) m -> p kb m", p=P))
+        def load_row(vec, name):
+            row = held.tile([P, C], F32, name=name)
+            nc.sync.dma_start(row[:], vec.rearrange("c o -> (o c)").partition_broadcast(P))
+            return row
+
+        def load_weight(w, name):
+            w_sb = held.tile([P, CB, C], BF16, name=name)
+            nc.sync.dma_start(w_sb[:], w.rearrange("(kb p) m -> p kb m", p=P))
+            return w_sb
 
         pos_of = {0: load_pos(0)}
+        tok = [held.tile([P, VOCAB], F32, name="tok%d" % b) for b in range(CB)]
         for b in range(CB):
             nc.sync.dma_start(tok[b][:], tok_emb[b * P : (b + 1) * P, :])
-        load_weight("wq", wq)
-        load_weight("wk", wk)
-        load_weight("wv", wv)
+        gain_row = load_row(gain_e, "gain_row")
+        bias_row = load_row(bias_e, "bias_row")
+        wq_sb = load_weight(wq, "wq_sb")
+        wk_sb = load_weight(wk, "wk_sb")
+        wv_sb = load_weight(wv, "wv_sb")
         pos_of[1] = load_pos(1)
-        load_weight("wo", wo)
+        wo_sb = load_weight(wo, "wo_sb")
 
-        per_channel = {}
+        gain1_sb = held.tile([P, CB], F32, name="gain1_sb")
+        bias1_sb = held.tile([P, CB], F32, name="bias1_sb")
         with nc.allow_non_contiguous_dma(reason="four values to a partition"):
-            for name, vec in (("gain_e", gain_e), ("bias_e", bias_e), ("gain1", gain1), ("bias1", bias1)):
-                per_channel[name] = held.tile([P, CB], F32, name=name + "_sb")
-                nc.scalar.dma_start(per_channel[name][:], vec.rearrange("(b p) o -> p (b o)", p=P))
-        gain_row = held.tile([P, C], F32, name="gain_row")
-        nc.scalar.dma_start(gain_row[:], gain_e.rearrange("c o -> (o c)").partition_broadcast(P))
-        bias_row = held.tile([P, C], F32, name="bias_row")
-        nc.scalar.dma_start(bias_row[:], bias_e.rearrange("c o -> (o c)").partition_broadcast(P))
+            nc.scalar.dma_start(gain1_sb[:], gain1.rearrange("(b p) o -> p (b o)", p=P))
+            nc.scalar.dma_start(bias1_sb[:], bias1.rearrange("(b p) o -> p (b o)", p=P))
 
         ident_f32 = held.tile([P, P], F32, name="ident_f32")
         make_identity(nc, ident_f32[:])
@@ -119,7 +129,7 @@ def tile_proteintransformer_b_kernel(
                 nc.tensor.transpose(back_ps[:, b, :], z[:, b * P : (b + 1) * P], ident_f32[:])
             return back_ps
 
-        def embed_norm_1(j):
+        def flip_embedding(j):
             emb = lookup(j)
             eT_ps = flip_ps.tile([P, C], F32, name="eT_ps")
             for b in range(CB):
@@ -129,7 +139,7 @@ def tile_proteintransformer_b_kernel(
             nc.vector.scalar_tensor_tensor(res[:], eT_ps[:], moments_of[j][0][:, 0:1], gain_row[:], ALU.subtract, ALU.mult)
             res_of[j] = res
 
-        def embed_norm_2(j):
+        def finish_x(j):
             ch, t = divmod(j, TB)
             if t == 0:
                 x_of[ch] = chunkp.tile([P, CB, CHUNK], BF16, name="x_bf")
@@ -146,20 +156,20 @@ def tile_proteintransformer_b_kernel(
                     chunkp.tile([P, TB, C], BF16, name="v_tok"),
                 )
             x_bf = x_of[ch]
-            which, i = divmod(g, CB)
+            kind, i = divmod(g, CB)
+            part = slice(i * P, (i + 1) * P)
             acc = qkv_ps.tile([P, CHUNK], F32, name="acc")
             for kb in range(CB):
-                if which < 2:
-                    w_sb = weights[("wq", "wk")[which]]
-                    nc.tensor.matmul(
-                        acc[:], w_sb[:, kb, i * P : (i + 1) * P], x_bf[:, kb, :], start=(kb == 0), stop=(kb == CB - 1)
-                    )
+                if kind == 0:
+                    nc.tensor.matmul(acc[:], wq_sb[:, kb, part], x_bf[:, kb, :], start=(kb == 0), stop=(kb == CB - 1))
+                elif kind == 1:
+                    nc.tensor.matmul(acc[:], wk_sb[:, kb, part], x_bf[:, kb, :], start=(kb == 0), stop=(kb == CB - 1))
                 else:
-                    nc.tensor.matmul(
-                        acc[:], x_bf[:, kb, i * P : (i + 1) * P], weights["wv"][:, kb, :],
-                        start=(kb == 0), stop=(kb == CB - 1),
-                    )
-            nc.scalar.mul(qkv_of[ch][which][:, i, :], acc[:], SCALE if which == 0 else 1.0)
+                    nc.tensor.matmul(acc[:], x_bf[:, kb, part], wv_sb[:, kb, :], start=(kb == 0), stop=(kb == CB - 1))
+            if kind == 0:
+                nc.scalar.mul(qkv_of[ch][kind][:, i, :], acc[:], SCALE)
+            else:
+                nc.scalar.copy(qkv_of[ch][kind][:, i, :], acc[:])
 
         def scores(j):
             ch, t = divmod(j, TB)
@@ -205,11 +215,11 @@ def tile_proteintransformer_b_kernel(
             ctx_bf = ctx_of[j]
             yT_ps = flip_ps.tile([P, C], F32, name="yT_ps")
             for kb in range(CB):
-                nc.tensor.matmul(yT_ps[:], ctx_bf[:, kb, :], weights["wo"][:, kb, :], start=(kb == 0), stop=(kb == CB - 1))
+                nc.tensor.matmul(yT_ps[:], ctx_bf[:, kb, :], wo_sb[:, kb, :], start=(kb == 0), stop=(kb == CB - 1))
             nc.vector.tensor_tensor(res_of[j][:], yT_ps[:], res_of[j][:], ALU.add)
             moments(j, res_of[j][:])
 
-        def final_norm(j):
+        def finish_out(j):
             mean_var, rstd = moments_of[j]
             zn = blockp.tile([P, C], F32, name="zn")
             nc.vector.tensor_scalar(zn[:], res_of[j][:], mean_var[:, 0:1], rstd[:], ALU.subtract, ALU.mult)
@@ -217,8 +227,7 @@ def tile_proteintransformer_b_kernel(
             done = blockp.tile([P, CB, P], F32, name="done")
             for b in range(CB):
                 nc.scalar.activation(
-                    done[:, b, :], zn_ps[:, b, :], ACT.Identity,
-                    bias=per_channel["bias1"][:, b : b + 1], scale=per_channel["gain1"][:, b : b + 1],
+                    done[:, b, :], zn_ps[:, b, :], ACT.Identity, bias=bias1_sb[:, b : b + 1], scale=gain1_sb[:, b : b + 1]
                 )
             nc.sync.dma_start(out_view[:, :, j * P : (j + 1) * P], done[:])
 
@@ -226,13 +235,13 @@ def tile_proteintransformer_b_kernel(
             if 0 <= j < NBLK:
                 stage(j)
 
-        for s in range(-5, NBLK + 7):
-            if_block(embed_norm_2, s + 4)
-            if_block(final_norm, s - 6)
-            if_block(context, s - 4)
-            if_block(residual, s - 5)
-            if_block(embed_norm_1, s + 5)
-            if_block(scores, s - 3)
+        for s in range(-FLIP_AHEAD, NBLK + OUT_BEHIND):
+            if_block(finish_x, s + NORM_AHEAD)
+            if_block(finish_out, s - OUT_BEHIND)
+            if_block(context, s - CONTEXT_BEHIND)
+            if_block(residual, s - RESIDUAL_BEHIND)
+            if_block(flip_embedding, s + FLIP_AHEAD)
+            if_block(scores, s - SCORES_BEHIND)
             if 0 <= s < NBLK:
                 for g in range((s % TB) * PER_STEP, (s % TB + 1) * PER_STEP):
                     project(s // TB, g)

@@ -16,20 +16,14 @@ VOCAB = 4096
 N = 2048
 CB = C // P
 NBLK = N // P
-CHUNK = 512
-NCHUNK = N // CHUNK
-TB = CHUNK // P
+POS_BLOCKS = 4
+POS_WIDTH = POS_BLOCKS * P
 EPS = 1e-5
 SCALE = 1.0 / math.sqrt(P)
 
-PER_STEP = 3 * CB // TB
-NORM_AHEAD = TB
-FLIP_AHEAD = NORM_AHEAD + 1
-SCORES_BEHIND = 2 * CB // PER_STEP + 1
-CONTEXT_BEHIND = SCORES_BEHIND + 1
-RESIDUAL_BEHIND = CONTEXT_BEHIND + 1
-OUT_BEHIND = RESIDUAL_BEHIND + 1
-RES_BUFS = FLIP_AHEAD + OUT_BEHIND + 1 + 2
+FIRST_AHEAD = 3
+LAST_BEHIND = 4
+RES_BUFS = FIRST_AHEAD + LAST_BEHIND + 1
 
 FLOPS = 4 * 2 * C * C * N + 2 * 2 * P * P * P * CB * NBLK
 
@@ -40,12 +34,12 @@ def tile_proteintransformer_b_kernel(
     nc = tc.nc
     with (
         tc.tile_pool(name="held", bufs=1) as held,
-        tc.tile_pool(name="chunkp", bufs=2) as chunkp,
+        tc.tile_pool(name="posp", bufs=2) as posp,
         tc.tile_pool(name="resp", bufs=RES_BUFS) as resp,
         tc.tile_pool(name="blockp", bufs=3) as blockp,
-        tc.psum_pool(name="flip_ps", bufs=1) as flip_ps,
-        tc.psum_pool(name="qkv_ps", bufs=2) as qkv_ps,
-        tc.psum_pool(name="score_ps", bufs=2) as score_ps,
+        tc.tile_pool(name="valuep", bufs=4) as valuep,
+        tc.psum_pool(name="one_ps", bufs=1) as one_ps,
+        tc.psum_pool(name="qkv_ps", bufs=3) as qkv_ps,
     ):
         offsets = held.tile([P, N // 16], U16, name="offsets")
         nc.sync.dma_start(offsets[:], offs)
@@ -53,9 +47,9 @@ def tile_proteintransformer_b_kernel(
         pos_view = pos_emb.rearrange("(b p) n -> p b n", p=P)
         out_view = out.rearrange("(b p) n -> p b n", p=P)
 
-        def load_pos(ch):
-            pos = chunkp.tile([P, CB, CHUNK], F32, name="pos")
-            nc.sync.dma_start(pos[:], pos_view[:, :, ch * CHUNK : (ch + 1) * CHUNK])
+        def load_pos(part):
+            pos = posp.tile([P, CB, POS_WIDTH], F32, name="pos")
+            nc.sync.dma_start(pos[:], pos_view[:, :, part * POS_WIDTH : (part + 1) * POS_WIDTH])
             return pos
 
         def load_row(vec, name):
@@ -93,155 +87,222 @@ def tile_proteintransformer_b_kernel(
         minus_half = held.tile([P, 1], F32, name="minus_half")
         nc.vector.memset(minus_half[:], -0.5)
 
-        x_of = {}
-        qkv_of = {}
-        moments_of = {}
-        res_of = {}
-        a_of = {}
-        ctx_of = {}
+        tile_of = {}
 
-        def lookup(j):
-            ch, t = divmod(j, TB)
-            emb = blockp.tile([P, CB, P], F32, name="emb")
-            piece = offsets[:, j * (P // 16) : (j + 1) * (P // 16)]
-            for b in range(CB):
-                nc.vector.tensor_tensor(
-                    emb[:, b, :], tok[b][:].indirect(piece), pos_of[ch][:, b, t * P : (t + 1) * P], ALU.add
-                )
-            if t == TB - 1 and ch + 2 < NCHUNK:
-                pos_of[ch + 2] = load_pos(ch + 2)
-            return emb
-
-        def moments(j, z):
-            stats = blockp.tile([P, 6], F32, name="stats")
+        def moments(j, z, norm):
+            stats = blockp.tile([P, 6], F32, name="stats" + norm)
             nc.vector.bn_stats(stats[:], z)
-            mean_var = blockp.tile([P, 2], F32, name="mean_var")
+            mean_var = blockp.tile([P, 2], F32, name="mean_var" + norm)
             nc.vector.bn_aggr(mean_var[:], stats[:])
-            var_eps = blockp.tile([P, 1], F32, name="var_eps")
+            var_eps = blockp.tile([P, 1], F32, name="var_eps" + norm)
             nc.vector.tensor_scalar_add(var_eps[:], mean_var[:, 1:2], EPS)
-            rstd = blockp.tile([P, 1], F32, name="rstd")
+            rstd = blockp.tile([P, 1], F32, name="rstd" + norm)
             nc.gpsimd.tensor_tensor(rstd[:], var_eps[:], minus_half[:], ALU.pow)
-            moments_of[j] = (mean_var, rstd)
+            tile_of["mean_var" + norm, j] = mean_var
+            tile_of["rstd" + norm, j] = rstd
 
-        def flip_back(z):
-            back_ps = flip_ps.tile([P, CB, P], F32, name="back_ps")
+        def flip_back(z, norm):
+            back_ps = one_ps.tile([P, CB, P], F32, name="back_ps" + norm)
             for b in range(CB):
                 nc.tensor.transpose(back_ps[:, b, :], z[:, b * P : (b + 1) * P], ident_f32[:])
             return back_ps
 
-        def flip_embedding(j):
-            emb = lookup(j)
-            eT_ps = flip_ps.tile([P, C], F32, name="eT_ps")
+        def look_up(j):
+            part, t = divmod(j, POS_BLOCKS)
+            emb = blockp.tile([P, CB, P], F32, name="emb")
+            piece = offsets[:, j * (P // 16) : (j + 1) * (P // 16)]
             for b in range(CB):
-                nc.tensor.transpose(eT_ps[:, b * P : (b + 1) * P], emb[:, b, :], ident_f32[:])
-            moments(j, eT_ps[:])
+                nc.vector.tensor_tensor(
+                    emb[:, b, :], tok[b][:].indirect(piece), pos_of[part][:, b, t * P : (t + 1) * P], ALU.add
+                )
+            if t == POS_BLOCKS - 1 and (part + 2) * POS_BLOCKS < NBLK:
+                pos_of[part + 2] = load_pos(part + 2)
+            tile_of["emb", j] = emb
+
+        def flip_e(j):
+            eT_ps = one_ps.tile([P, C], F32, name="eT_ps", tag="e_or_s")
+            for b in range(CB):
+                nc.tensor.transpose(eT_ps[:, b * P : (b + 1) * P], tile_of["emb", j][:, b, :], ident_f32[:])
+            tile_of["eT_ps", j] = eT_ps
+
+        def centre_e(j):
+            eT_ps = tile_of["eT_ps", j]
+            moments(j, eT_ps[:], "_e")
             res = resp.tile([P, C], F32, name="res")
-            nc.vector.scalar_tensor_tensor(res[:], eT_ps[:], moments_of[j][0][:, 0:1], gain_row[:], ALU.subtract, ALU.mult)
-            res_of[j] = res
+            nc.vector.scalar_tensor_tensor(
+                res[:], eT_ps[:], tile_of["mean_var_e", j][:, 0:1], gain_row[:], ALU.subtract, ALU.mult
+            )
+            tile_of["res", j] = res
 
         def finish_x(j):
-            ch, t = divmod(j, TB)
-            if t == 0:
-                x_of[ch] = chunkp.tile([P, CB, CHUNK], BF16, name="x_bf")
-            res = res_of[j]
-            nc.vector.scalar_tensor_tensor(res[:], res[:], moments_of[j][1][:], bias_row[:], ALU.mult, ALU.add)
-            x_ps = flip_back(res)
-            nc.scalar.copy(x_of[ch][:, :, t * P : (t + 1) * P], x_ps[:])
+            res = tile_of["res", j]
+            nc.vector.scalar_tensor_tensor(res[:], res[:], tile_of["rstd_e", j][:], bias_row[:], ALU.mult, ALU.add)
 
-        def project(ch, g):
-            if g == 0:
-                qkv_of[ch] = (
-                    chunkp.tile([P, CB, CHUNK], BF16, name="q_bf"),
-                    chunkp.tile([P, CB, CHUNK], BF16, name="k_bf"),
-                    chunkp.tile([P, TB, C], BF16, name="v_tok"),
-                )
-            x_bf = x_of[ch]
-            kind, i = divmod(g, CB)
-            part = slice(i * P, (i + 1) * P)
-            acc = qkv_ps.tile([P, CHUNK], F32, name="acc")
+        def flip_x(j):
+            tile_of["x_ps", j] = flip_back(tile_of["res", j], "_e")
+
+        def round_x(j):
+            x_bf = blockp.tile([P, CB, P], BF16, name="x_bf")
+            nc.scalar.copy(x_bf[:], tile_of["x_ps", j][:])
+            tile_of["x_bf", j] = x_bf
+
+        def project_heads(j, w_sb, name):
+            x_bf = tile_of["x_bf", j]
+            acc = qkv_ps.tile([P, C], F32, name="acc")
+            for h in range(CB):
+                head = slice(h * P, (h + 1) * P)
+                for kb in range(CB):
+                    nc.tensor.matmul(acc[:, head], w_sb[:, kb, head], x_bf[:, kb, :], start=(kb == 0), stop=(kb == CB - 1))
+            tile_of[name + "_ps", j] = acc
+
+        def project_q(j):
+            project_heads(j, wq_sb, "q")
+
+        def project_k(j):
+            project_heads(j, wk_sb, "k")
+
+        def project_v(j):
+            x_bf = tile_of["x_bf", j]
+            acc = qkv_ps.tile([P, C], F32, name="acc")
             for kb in range(CB):
-                if kind == 0:
-                    nc.tensor.matmul(acc[:], wq_sb[:, kb, part], x_bf[:, kb, :], start=(kb == 0), stop=(kb == CB - 1))
-                elif kind == 1:
-                    nc.tensor.matmul(acc[:], wk_sb[:, kb, part], x_bf[:, kb, :], start=(kb == 0), stop=(kb == CB - 1))
-                else:
-                    nc.tensor.matmul(acc[:], x_bf[:, kb, part], wv_sb[:, kb, :], start=(kb == 0), stop=(kb == CB - 1))
-            if kind == 0:
-                nc.scalar.mul(qkv_of[ch][kind][:, i, :], acc[:], SCALE)
-            else:
-                nc.scalar.copy(qkv_of[ch][kind][:, i, :], acc[:])
+                nc.tensor.matmul(acc[:], x_bf[:, kb, :], wv_sb[:, kb, :], start=(kb == 0), stop=(kb == CB - 1))
+            tile_of["v_ps", j] = acc
+
+        def round_q(j):
+            q_bf = blockp.tile([P, C], BF16, name="q_bf")
+            nc.scalar.mul(q_bf[:], tile_of["q_ps", j][:], SCALE)
+            tile_of["q_bf", j] = q_bf
+
+        def round_k(j):
+            k_bf = blockp.tile([P, C], BF16, name="k_bf")
+            nc.scalar.copy(k_bf[:], tile_of["k_ps", j][:])
+            tile_of["k_bf", j] = k_bf
+
+        def round_v(j):
+            v_bf = valuep.tile([P, C], BF16, name="v_bf")
+            nc.scalar.copy(v_bf[:], tile_of["v_ps", j][:])
+            tile_of["v_bf", j] = v_bf
 
         def scores(j):
-            ch, t = divmod(j, TB)
-            blk = slice(t * P, (t + 1) * P)
-            q_bf, k_bf = qkv_of[ch][0], qkv_of[ch][1]
-            s_ps = score_ps.tile([P, CB, P], F32, name="s_ps")
+            s_ps = one_ps.tile([P, CB, P], F32, name="s_ps", tag="e_or_s")
             for h in range(CB):
-                nc.tensor.matmul(s_ps[:, h, :], q_bf[:, h, blk], k_bf[:, h, blk], start=True, stop=True)
+                head = slice(h * P, (h + 1) * P)
+                nc.tensor.matmul(s_ps[:, h, :], tile_of["q_bf", j][:, head], tile_of["k_bf", j][:, head], start=True, stop=True)
+            tile_of["s_ps", j] = s_ps
+
+        def row_max(j):
             neg_top = blockp.tile([P, CB], F32, name="neg_top")
-            nc.vector.reduce_max(neg_top[:], s_ps[:], axis=AX.X, negate=True)
+            nc.vector.reduce_max(neg_top[:], tile_of["s_ps", j][:], axis=AX.X, negate=True)
+            tile_of["neg_top", j] = neg_top
+
+        def exponentials(j):
             expo = blockp.tile([P, CB, P], F32, name="expo")
             total = blockp.tile([P, CB], F32, name="total")
             for h in range(CB):
                 nc.scalar.activation(
-                    expo[:, h, :], s_ps[:, h, :], ACT.Exp,
-                    bias=neg_top[:, h : h + 1], accum_out=total[:, h : h + 1],
+                    expo[:, h, :], tile_of["s_ps", j][:, h, :], ACT.Exp,
+                    bias=tile_of["neg_top", j][:, h : h + 1], accum_out=total[:, h : h + 1],
                 )
+            tile_of["expo", j] = expo
+            tile_of["total", j] = total
+
+        def invert_sums(j):
             inv = blockp.tile([P, CB], F32, name="inv")
-            nc.vector.reciprocal(inv[:], total[:])
+            nc.vector.reciprocal(inv[:], tile_of["total", j][:])
+            tile_of["inv", j] = inv
+
+        def weights(j):
             a_bf = blockp.tile([P, CB, P], BF16, name="a_bf")
             for h in range(CB):
-                nc.scalar.activation(a_bf[:, h, :], expo[:, h, :], ACT.Copy, scale=inv[:, h : h + 1])
-            a_of[j] = a_bf
+                nc.scalar.activation(
+                    a_bf[:, h, :], tile_of["expo", j][:, h, :], ACT.Copy, scale=tile_of["inv", j][:, h : h + 1]
+                )
+            tile_of["a_bf", j] = a_bf
+
+        def flip_weights(j):
+            flip_ctx = one_ps.tile([P, 2, CB, P], BF16, name="flip_ctx")
+            for h in range(CB):
+                nc.tensor.transpose(flip_ctx[:, 0, h, :], tile_of["a_bf", j][:, h, :], ident_bf[:])
+            tile_of["flip_ctx", j] = flip_ctx
+
+        def copy_weights(j):
+            aT_bf = blockp.tile([P, CB, P], BF16, name="aT_bf")
+            nc.scalar.copy(aT_bf[:], tile_of["flip_ctx", j][:, 0, :, :])
+            tile_of["aT_bf", j] = aT_bf
 
         def context(j):
-            ch, t = divmod(j, TB)
-            v_tok = qkv_of[ch][2]
-            a_bf = a_of[j]
-            flip_ctx = flip_ps.tile([P, 2, CB, P], BF16, name="flip_ctx")
-            for h in range(CB):
-                nc.tensor.transpose(flip_ctx[:, 0, h, :], a_bf[:, h, :], ident_bf[:])
-            aT_bf = blockp.tile([P, CB, P], BF16, name="aT_bf")
-            nc.scalar.copy(aT_bf[:], flip_ctx[:, 0, :, :])
             for h in range(CB):
                 nc.tensor.matmul(
-                    flip_ctx[:, 1, h, :], v_tok[:, t, h * P : (h + 1) * P], aT_bf[:, h, :], start=True, stop=True
+                    tile_of["flip_ctx", j][:, 1, h, :], tile_of["v_bf", j][:, h * P : (h + 1) * P], tile_of["aT_bf", j][:, h, :],
+                    start=True, stop=True,
                 )
+
+        def copy_context(j):
             ctx_bf = blockp.tile([P, CB, P], BF16, name="ctx_bf")
-            nc.scalar.copy(ctx_bf[:], flip_ctx[:, 1, :, :])
-            ctx_of[j] = ctx_bf
+            nc.scalar.copy(ctx_bf[:], tile_of["flip_ctx", j][:, 1, :, :])
+            tile_of["ctx_bf", j] = ctx_bf
 
-        def residual(j):
-            ctx_bf = ctx_of[j]
-            yT_ps = flip_ps.tile([P, C], F32, name="yT_ps")
+        def project_out(j):
+            yT_ps = one_ps.tile([P, C], F32, name="yT_ps")
             for kb in range(CB):
-                nc.tensor.matmul(yT_ps[:], ctx_bf[:, kb, :], wo_sb[:, kb, :], start=(kb == 0), stop=(kb == CB - 1))
-            nc.vector.tensor_tensor(res_of[j][:], yT_ps[:], res_of[j][:], ALU.add)
-            moments(j, res_of[j][:])
+                nc.tensor.matmul(yT_ps[:], tile_of["ctx_bf", j][:, kb, :], wo_sb[:, kb, :], start=(kb == 0), stop=(kb == CB - 1))
+            tile_of["yT_ps", j] = yT_ps
 
-        def finish_out(j):
-            mean_var, rstd = moments_of[j]
+        def add_residual(j):
+            res = tile_of["res", j]
+            nc.vector.tensor_tensor(res[:], tile_of["yT_ps", j][:], res[:], ALU.add)
+
+        def moments_y(j):
+            moments(j, tile_of["res", j][:], "_y")
+
+        def normalise_y(j):
             zn = blockp.tile([P, C], F32, name="zn")
-            nc.vector.tensor_scalar(zn[:], res_of[j][:], mean_var[:, 0:1], rstd[:], ALU.subtract, ALU.mult)
-            zn_ps = flip_back(zn)
+            nc.vector.tensor_scalar(
+                zn[:], tile_of["res", j][:], tile_of["mean_var_y", j][:, 0:1], tile_of["rstd_y", j][:], ALU.subtract, ALU.mult
+            )
+            tile_of["zn", j] = zn
+
+        def flip_out(j):
+            tile_of["zn_ps", j] = flip_back(tile_of["zn", j], "_y")
+
+        def store(j):
             done = blockp.tile([P, CB, P], F32, name="done")
             for b in range(CB):
                 nc.scalar.activation(
-                    done[:, b, :], zn_ps[:, b, :], ACT.Identity, bias=bias1_sb[:, b : b + 1], scale=gain1_sb[:, b : b + 1]
+                    done[:, b, :], tile_of["zn_ps", j][:, b, :], ACT.Identity,
+                    bias=bias1_sb[:, b : b + 1], scale=gain1_sb[:, b : b + 1],
                 )
             nc.sync.dma_start(out_view[:, :, j * P : (j + 1) * P], done[:])
 
-        def if_block(stage, j):
+        def at(piece, j):
             if 0 <= j < NBLK:
-                stage(j)
+                piece(j)
 
-        for s in range(-FLIP_AHEAD, NBLK + OUT_BEHIND):
-            if_block(finish_x, s + NORM_AHEAD)
-            if_block(finish_out, s - OUT_BEHIND)
-            if_block(context, s - CONTEXT_BEHIND)
-            if_block(residual, s - RESIDUAL_BEHIND)
-            if_block(flip_embedding, s + FLIP_AHEAD)
-            if_block(scores, s - SCORES_BEHIND)
-            if 0 <= s < NBLK:
-                for g in range((s % TB) * PER_STEP, (s % TB + 1) * PER_STEP):
-                    project(s // TB, g)
+        for s in range(-FIRST_AHEAD, NBLK + LAST_BEHIND):
+            at(add_residual, s - 4)
+            at(project_q, s)
+            at(row_max, s - 1)
+            at(moments_y, s - 4)
+            at(flip_weights, s - 2)
+            at(exponentials, s - 1)
+            at(flip_x, s + 1)
+            at(project_k, s)
+            at(copy_weights, s - 2)
+            at(invert_sums, s - 1)
+            at(look_up, s + 3)
+            at(round_q, s)
+            at(flip_e, s + 2)
+            at(context, s - 2)
+            at(weights, s - 1)
+            at(normalise_y, s - 4)
+            at(project_v, s)
+            at(centre_e, s + 2)
+            at(round_x, s + 1)
+            at(round_k, s)
+            at(flip_out, s - 4)
+            at(project_out, s - 3)
+            at(copy_context, s - 2)
+            at(finish_x, s + 2)
+            at(round_v, s)
+            at(scores, s)
+            at(store, s - 4)

@@ -16,8 +16,7 @@ VOCAB = 4096
 N = 2048
 CB = C // P
 NBLK = N // P
-POS_BLOCKS = 4
-POS_WIDTH = POS_BLOCKS * P
+POS_AHEAD = 4
 EPS = 1e-5
 SCALE = 1.0 / math.sqrt(P)
 
@@ -34,23 +33,25 @@ def tile_proteintransformer_b_kernel(
     nc = tc.nc
     with (
         tc.tile_pool(name="held", bufs=1) as held,
-        tc.tile_pool(name="posp", bufs=2) as posp,
+        tc.tile_pool(name="posp", bufs=POS_AHEAD + 1) as posp,
         tc.tile_pool(name="resp", bufs=RES_BUFS) as resp,
         tc.tile_pool(name="blockp", bufs=3) as blockp,
         tc.tile_pool(name="valuep", bufs=4) as valuep,
         tc.psum_pool(name="one_ps", bufs=1) as one_ps,
-        tc.psum_pool(name="qkv_ps", bufs=3) as qkv_ps,
+        tc.psum_pool(name="wide_ps", bufs=3) as wide_ps,
     ):
+        tile_of = {}
+
         offsets = held.tile([P, N // 16], U16, name="offsets")
         nc.sync.dma_start(offsets[:], offs)
 
         pos_view = pos_emb.rearrange("(b p) n -> p b n", p=P)
         out_view = out.rearrange("(b p) n -> p b n", p=P)
 
-        def load_pos(part):
-            pos = posp.tile([P, CB, POS_WIDTH], F32, name="pos")
-            nc.sync.dma_start(pos[:], pos_view[:, :, part * POS_WIDTH : (part + 1) * POS_WIDTH])
-            return pos
+        def load_pos(j):
+            pos = posp.tile([P, CB, P], F32, name="pos")
+            nc.sync.dma_start(pos[:], pos_view[:, :, j * P : (j + 1) * P])
+            tile_of["pos", j] = pos
 
         def load_row(vec, name):
             row = held.tile([P, C], F32, name=name)
@@ -62,16 +63,18 @@ def tile_proteintransformer_b_kernel(
             nc.sync.dma_start(w_sb[:], w.rearrange("(kb p) m -> p kb m", p=P))
             return w_sb
 
-        pos_of = {0: load_pos(0)}
+        load_pos(0)
         tok = [held.tile([P, VOCAB], F32, name="tok%d" % b) for b in range(CB)]
         for b in range(CB):
             nc.sync.dma_start(tok[b][:], tok_emb[b * P : (b + 1) * P, :])
         gain_row = load_row(gain_e, "gain_row")
+        load_pos(1)
         bias_row = load_row(bias_e, "bias_row")
         wq_sb = load_weight(wq, "wq_sb")
+        load_pos(2)
         wk_sb = load_weight(wk, "wk_sb")
         wv_sb = load_weight(wv, "wv_sb")
-        pos_of[1] = load_pos(1)
+        load_pos(3)
         wo_sb = load_weight(wo, "wo_sb")
 
         gain1_sb = held.tile([P, CB], F32, name="gain1_sb")
@@ -87,8 +90,6 @@ def tile_proteintransformer_b_kernel(
         minus_half = held.tile([P, 1], F32, name="minus_half")
         nc.vector.memset(minus_half[:], -0.5)
 
-        tile_of = {}
-
         def moments(j, z, norm):
             stats = blockp.tile([P, 6], F32, name="stats" + norm)
             nc.vector.bn_stats(stats[:], z)
@@ -101,26 +102,23 @@ def tile_proteintransformer_b_kernel(
             tile_of["mean_var" + norm, j] = mean_var
             tile_of["rstd" + norm, j] = rstd
 
-        def flip_back(z, norm):
-            back_ps = one_ps.tile([P, CB, P], F32, name="back_ps" + norm)
+        def flip_back(z, tag):
+            back_ps = one_ps.tile([P, CB, P], F32, name="back_ps", tag=tag)
             for b in range(CB):
                 nc.tensor.transpose(back_ps[:, b, :], z[:, b * P : (b + 1) * P], ident_f32[:])
             return back_ps
 
         def look_up(j):
-            part, t = divmod(j, POS_BLOCKS)
             emb = blockp.tile([P, CB, P], F32, name="emb")
             piece = offsets[:, j * (P // 16) : (j + 1) * (P // 16)]
             for b in range(CB):
-                nc.vector.tensor_tensor(
-                    emb[:, b, :], tok[b][:].indirect(piece), pos_of[part][:, b, t * P : (t + 1) * P], ALU.add
-                )
-            if t == POS_BLOCKS - 1 and (part + 2) * POS_BLOCKS < NBLK:
-                pos_of[part + 2] = load_pos(part + 2)
+                nc.vector.tensor_tensor(emb[:, b, :], tok[b][:].indirect(piece), tile_of["pos", j][:, b, :], ALU.add)
+            if j + POS_AHEAD < NBLK:
+                load_pos(j + POS_AHEAD)
             tile_of["emb", j] = emb
 
         def flip_e(j):
-            eT_ps = one_ps.tile([P, C], F32, name="eT_ps", tag="e_or_s")
+            eT_ps = one_ps.tile([P, C], F32, name="eT_ps")
             for b in range(CB):
                 nc.tensor.transpose(eT_ps[:, b * P : (b + 1) * P], tile_of["emb", j][:, b, :], ident_f32[:])
             tile_of["eT_ps", j] = eT_ps
@@ -139,7 +137,7 @@ def tile_proteintransformer_b_kernel(
             nc.vector.scalar_tensor_tensor(res[:], res[:], tile_of["rstd_e", j][:], bias_row[:], ALU.mult, ALU.add)
 
         def flip_x(j):
-            tile_of["x_ps", j] = flip_back(tile_of["res", j], "_e")
+            tile_of["x_ps", j] = flip_back(tile_of["res", j], "x_ps")
 
         def round_x(j):
             x_bf = blockp.tile([P, CB, P], BF16, name="x_bf")
@@ -148,7 +146,7 @@ def tile_proteintransformer_b_kernel(
 
         def project_heads(j, w_sb, name):
             x_bf = tile_of["x_bf", j]
-            acc = qkv_ps.tile([P, C], F32, name="acc")
+            acc = wide_ps.tile([P, C], F32, name="acc")
             for h in range(CB):
                 head = slice(h * P, (h + 1) * P)
                 for kb in range(CB):
@@ -163,7 +161,7 @@ def tile_proteintransformer_b_kernel(
 
         def project_v(j):
             x_bf = tile_of["x_bf", j]
-            acc = qkv_ps.tile([P, C], F32, name="acc")
+            acc = wide_ps.tile([P, C], F32, name="acc")
             for kb in range(CB):
                 nc.tensor.matmul(acc[:], x_bf[:, kb, :], wv_sb[:, kb, :], start=(kb == 0), stop=(kb == CB - 1))
             tile_of["v_ps", j] = acc
@@ -184,7 +182,7 @@ def tile_proteintransformer_b_kernel(
             tile_of["v_bf", j] = v_bf
 
         def scores(j):
-            s_ps = one_ps.tile([P, CB, P], F32, name="s_ps", tag="e_or_s")
+            s_ps = one_ps.tile([P, CB, P], F32, name="s_ps")
             for h in range(CB):
                 head = slice(h * P, (h + 1) * P)
                 nc.tensor.matmul(s_ps[:, h, :], tile_of["q_bf", j][:, head], tile_of["k_bf", j][:, head], start=True, stop=True)
@@ -239,11 +237,11 @@ def tile_proteintransformer_b_kernel(
 
         def copy_context(j):
             ctx_bf = blockp.tile([P, CB, P], BF16, name="ctx_bf")
-            nc.scalar.copy(ctx_bf[:], tile_of["flip_ctx", j][:, 1, :, :])
+            nc.vector.tensor_copy(ctx_bf[:], tile_of["flip_ctx", j][:, 1, :, :])
             tile_of["ctx_bf", j] = ctx_bf
 
         def project_out(j):
-            yT_ps = one_ps.tile([P, C], F32, name="yT_ps")
+            yT_ps = wide_ps.tile([P, C], F32, name="yT_ps", tag="acc")
             for kb in range(CB):
                 nc.tensor.matmul(yT_ps[:], tile_of["ctx_bf", j][:, kb, :], wo_sb[:, kb, :], start=(kb == 0), stop=(kb == CB - 1))
             tile_of["yT_ps", j] = yT_ps
@@ -263,7 +261,7 @@ def tile_proteintransformer_b_kernel(
             tile_of["zn", j] = zn
 
         def flip_out(j):
-            tile_of["zn_ps", j] = flip_back(tile_of["zn", j], "_y")
+            tile_of["zn_ps", j] = flip_back(tile_of["zn", j], "out_ps")
 
         def store(j):
             done = blockp.tile([P, CB, P], F32, name="done")
@@ -279,30 +277,30 @@ def tile_proteintransformer_b_kernel(
                 piece(j)
 
         for s in range(-FIRST_AHEAD, NBLK + LAST_BEHIND):
-            at(add_residual, s - 4)
             at(project_q, s)
+            at(add_residual, s - 3)
             at(row_max, s - 1)
-            at(moments_y, s - 4)
-            at(flip_weights, s - 2)
-            at(exponentials, s - 1)
-            at(flip_x, s + 1)
-            at(project_k, s)
             at(copy_weights, s - 2)
+            at(project_k, s)
+            at(finish_x, s + 1)
+            at(exponentials, s - 1)
+            at(moments_y, s - 3)
+            at(round_q, s)
+            at(context, s - 2)
             at(invert_sums, s - 1)
             at(look_up, s + 3)
-            at(round_q, s)
-            at(flip_e, s + 2)
-            at(context, s - 2)
-            at(weights, s - 1)
-            at(normalise_y, s - 4)
             at(project_v, s)
+            at(flip_x, s + 1)
+            at(copy_context, s - 2)
+            at(weights, s - 1)
+            at(normalise_y, s - 3)
+            at(flip_e, s + 2)
+            at(flip_out, s - 4)
+            at(round_k, s)
+            at(project_out, s - 2)
             at(centre_e, s + 2)
             at(round_x, s + 1)
-            at(round_k, s)
-            at(flip_out, s - 4)
-            at(project_out, s - 3)
-            at(copy_context, s - 2)
-            at(finish_x, s + 2)
             at(round_v, s)
             at(scores, s)
+            at(flip_weights, s - 1)
             at(store, s - 4)

@@ -279,21 +279,21 @@ def tile_proteintransformer_b_kernel(
         for s in range(-FIRST_AHEAD, NBLK + LAST_BEHIND):
             at(project_q, s)
             at(add_residual, s - 3)
-            at(row_max, s - 1)
             at(copy_weights, s - 2)
+            at(moments_y, s - 3)
             at(project_k, s)
+            at(row_max, s - 1)
             at(finish_x, s + 1)
             at(exponentials, s - 1)
-            at(moments_y, s - 3)
             at(round_q, s)
             at(context, s - 2)
             at(invert_sums, s - 1)
-            at(look_up, s + 3)
             at(project_v, s)
             at(flip_x, s + 1)
             at(copy_context, s - 2)
             at(weights, s - 1)
             at(normalise_y, s - 3)
+            at(look_up, s + 3)
             at(flip_e, s + 2)
             at(flip_out, s - 4)
             at(round_k, s)

@@ -20,8 +20,9 @@ POS_AHEAD = 4
 EPS = 1e-5
 SCALE = 1.0 / math.sqrt(P)
 
-FIRST_AHEAD = 3
-LAST_BEHIND = 4
+FIRST_AHEAD = 4
+HELD_BACK = 3
+LAST_BEHIND = 5 + HELD_BACK
 RES_BUFS = FIRST_AHEAD + LAST_BEHIND + 1
 
 FLOPS = 4 * 2 * C * C * N + 2 * 2 * P * P * P * CB * NBLK
@@ -37,7 +38,9 @@ def tile_proteintransformer_b_kernel(
         tc.tile_pool(name="resp", bufs=RES_BUFS) as resp,
         tc.tile_pool(name="blockp", bufs=3) as blockp,
         tc.tile_pool(name="valuep", bufs=4) as valuep,
+        tc.tile_pool(name="ctxp", bufs=HELD_BACK + 2) as ctxp,
         tc.psum_pool(name="one_ps", bufs=1) as one_ps,
+        tc.psum_pool(name="two_ps", bufs=2) as two_ps,
         tc.psum_pool(name="wide_ps", bufs=3) as wide_ps,
     ):
         tile_of = {}
@@ -118,7 +121,7 @@ def tile_proteintransformer_b_kernel(
             tile_of["emb", j] = emb
 
         def flip_e(j):
-            eT_ps = one_ps.tile([P, C], F32, name="eT_ps")
+            eT_ps = two_ps.tile([P, C], F32, name="eT_ps", tag="e_or_s")
             for b in range(CB):
                 nc.tensor.transpose(eT_ps[:, b * P : (b + 1) * P], tile_of["emb", j][:, b, :], ident_f32[:])
             tile_of["eT_ps", j] = eT_ps
@@ -182,7 +185,7 @@ def tile_proteintransformer_b_kernel(
             tile_of["v_bf", j] = v_bf
 
         def scores(j):
-            s_ps = one_ps.tile([P, CB, P], F32, name="s_ps")
+            s_ps = two_ps.tile([P, CB, P], F32, name="s_ps", tag="e_or_s")
             for h in range(CB):
                 head = slice(h * P, (h + 1) * P)
                 nc.tensor.matmul(s_ps[:, h, :], tile_of["q_bf", j][:, head], tile_of["k_bf", j][:, head], start=True, stop=True)
@@ -236,7 +239,7 @@ def tile_proteintransformer_b_kernel(
                 )
 
         def copy_context(j):
-            ctx_bf = blockp.tile([P, CB, P], BF16, name="ctx_bf")
+            ctx_bf = ctxp.tile([P, CB, P], BF16, name="ctx_bf")
             nc.vector.tensor_copy(ctx_bf[:], tile_of["flip_ctx", j][:, 1, :, :])
             tile_of["ctx_bf", j] = ctx_bf
 
@@ -278,9 +281,9 @@ def tile_proteintransformer_b_kernel(
 
         for s in range(-FIRST_AHEAD, NBLK + LAST_BEHIND):
             at(project_q, s)
-            at(add_residual, s - 3)
+            at(add_residual, s - 3 - HELD_BACK)
             at(copy_weights, s - 2)
-            at(moments_y, s - 3)
+            at(moments_y, s - 3 - HELD_BACK)
             at(project_k, s)
             at(row_max, s - 1)
             at(finish_x, s + 1)
@@ -288,19 +291,19 @@ def tile_proteintransformer_b_kernel(
             at(round_q, s)
             at(context, s - 2)
             at(invert_sums, s - 1)
-            at(project_v, s)
             at(flip_x, s + 1)
+            at(project_v, s)
             at(copy_context, s - 2)
             at(weights, s - 1)
-            at(normalise_y, s - 3)
-            at(look_up, s + 3)
-            at(flip_e, s + 2)
-            at(flip_out, s - 4)
+            at(normalise_y, s - 4 - HELD_BACK)
+            at(look_up, s + 4)
+            at(flip_e, s + 3)
+            at(flip_out, s - 5 - HELD_BACK)
             at(round_k, s)
-            at(project_out, s - 2)
-            at(centre_e, s + 2)
+            at(project_out, s - 2 - HELD_BACK)
+            at(centre_e, s + 3)
             at(round_x, s + 1)
             at(round_v, s)
             at(scores, s)
             at(flip_weights, s - 1)
-            at(store, s - 4)
+            at(store, s - 5 - HELD_BACK)

@@ -21,8 +21,8 @@ EPS = 1e-5
 SCALE = 1.0 / math.sqrt(P)
 
 FIRST_AHEAD = 4
-HELD_BACK = 3
-LAST_BEHIND = 5 + HELD_BACK
+HELD_BACK = 2
+LAST_BEHIND = 6 + HELD_BACK
 RES_BUFS = FIRST_AHEAD + LAST_BEHIND + 1
 
 FLOPS = 4 * 2 * C * C * N + 2 * 2 * P * P * P * CB * NBLK
@@ -37,7 +37,7 @@ def tile_proteintransformer_b_kernel(
         tc.tile_pool(name="posp", bufs=POS_AHEAD + 1) as posp,
         tc.tile_pool(name="resp", bufs=RES_BUFS) as resp,
         tc.tile_pool(name="blockp", bufs=3) as blockp,
-        tc.tile_pool(name="valuep", bufs=4) as valuep,
+        tc.tile_pool(name="valuep", bufs=5) as valuep,
         tc.tile_pool(name="ctxp", bufs=HELD_BACK + 2) as ctxp,
         tc.psum_pool(name="one_ps", bufs=1) as one_ps,
         tc.psum_pool(name="two_ps", bufs=2) as two_ps,
@@ -281,29 +281,29 @@ def tile_proteintransformer_b_kernel(
 
         for s in range(-FIRST_AHEAD, NBLK + LAST_BEHIND):
             at(project_q, s)
-            at(add_residual, s - 3 - HELD_BACK)
-            at(copy_weights, s - 2)
-            at(moments_y, s - 3 - HELD_BACK)
+            at(add_residual, s - 4 - HELD_BACK)
+            at(copy_weights, s - 3)
+            at(moments_y, s - 4 - HELD_BACK)
             at(project_k, s)
-            at(row_max, s - 1)
+            at(row_max, s - 2)
             at(finish_x, s + 1)
-            at(exponentials, s - 1)
+            at(exponentials, s - 2)
             at(round_q, s)
-            at(context, s - 2)
-            at(invert_sums, s - 1)
+            at(context, s - 3)
+            at(invert_sums, s - 2)
             at(flip_x, s + 1)
             at(project_v, s)
-            at(copy_context, s - 2)
-            at(weights, s - 1)
-            at(normalise_y, s - 4 - HELD_BACK)
+            at(copy_context, s - 3)
+            at(weights, s - 2)
+            at(normalise_y, s - 5 - HELD_BACK)
             at(look_up, s + 4)
             at(flip_e, s + 3)
-            at(flip_out, s - 5 - HELD_BACK)
+            at(flip_out, s - 6 - HELD_BACK)
             at(round_k, s)
-            at(project_out, s - 2 - HELD_BACK)
+            at(project_out, s - 3 - HELD_BACK)
             at(centre_e, s + 3)
             at(round_x, s + 1)
             at(round_v, s)
-            at(scores, s)
-            at(flip_weights, s - 1)
-            at(store, s - 5 - HELD_BACK)
+            at(scores, s - 1)
+            at(flip_weights, s - 2)
+            at(store, s - 6 - HELD_BACK)

@@ -105,8 +105,8 @@ def tile_proteintransformer_b_kernel(
             tile_of["mean_var" + norm, j] = mean_var
             tile_of["rstd" + norm, j] = rstd
 
-        def flip_back(z, tag):
-            back_ps = one_ps.tile([P, CB, P], F32, name="back_ps", tag=tag)
+        def flip_back(z, pool, tag):
+            back_ps = pool.tile([P, CB, P], F32, name="back_ps", tag=tag)
             for b in range(CB):
                 nc.tensor.transpose(back_ps[:, b, :], z[:, b * P : (b + 1) * P], ident_f32[:])
             return back_ps
@@ -140,7 +140,7 @@ def tile_proteintransformer_b_kernel(
             nc.vector.scalar_tensor_tensor(res[:], res[:], tile_of["rstd_e", j][:], bias_row[:], ALU.mult, ALU.add)
 
         def flip_x(j):
-            tile_of["x_ps", j] = flip_back(tile_of["res", j], "x_ps")
+            tile_of["x_ps", j] = flip_back(tile_of["res", j], two_ps, "x_or_w")
 
         def round_x(j):
             x_bf = blockp.tile([P, CB, P], BF16, name="x_bf")
@@ -221,7 +221,7 @@ def tile_proteintransformer_b_kernel(
             tile_of["a_bf", j] = a_bf
 
         def flip_weights(j):
-            flip_ctx = one_ps.tile([P, 2, CB, P], BF16, name="flip_ctx")
+            flip_ctx = two_ps.tile([P, 2, CB, P], BF16, name="flip_ctx", tag="x_or_w")
             for h in range(CB):
                 nc.tensor.transpose(flip_ctx[:, 0, h, :], tile_of["a_bf", j][:, h, :], ident_bf[:])
             tile_of["flip_ctx", j] = flip_ctx
@@ -264,7 +264,7 @@ def tile_proteintransformer_b_kernel(
             tile_of["zn", j] = zn
 
         def flip_out(j):
-            tile_of["zn_ps", j] = flip_back(tile_of["zn", j], "out_ps")
+            tile_of["zn_ps", j] = flip_back(tile_of["zn", j], one_ps, "out_ps")
 
         def store(j):
             done = blockp.tile([P, CB, P], F32, name="done")
@@ -280,16 +280,18 @@ def tile_proteintransformer_b_kernel(
                 piece(j)
 
         for s in range(-FIRST_AHEAD, NBLK + LAST_BEHIND):
+            at(flip_e, s + 3)
             at(project_q, s)
             at(add_residual, s - 4 - HELD_BACK)
             at(copy_weights, s - 3)
             at(moments_y, s - 4 - HELD_BACK)
             at(project_k, s)
+            at(centre_e, s + 3)
             at(row_max, s - 2)
-            at(finish_x, s + 1)
             at(exponentials, s - 2)
             at(round_q, s)
             at(context, s - 3)
+            at(finish_x, s + 1)
             at(invert_sums, s - 2)
             at(flip_x, s + 1)
             at(project_v, s)
@@ -297,11 +299,9 @@ def tile_proteintransformer_b_kernel(
             at(weights, s - 2)
             at(normalise_y, s - 5 - HELD_BACK)
             at(look_up, s + 4)
-            at(flip_e, s + 3)
             at(flip_out, s - 6 - HELD_BACK)
             at(round_k, s)
             at(project_out, s - 3 - HELD_BACK)
-            at(centre_e, s + 3)
             at(round_x, s + 1)
             at(round_v, s)
             at(scores, s - 1)

@@ -23,7 +23,7 @@ SCALE = 1.0 / math.sqrt(P)
 FIRST_AHEAD = 4
 HELD_BACK = 2
 LAST_BEHIND = 6 + HELD_BACK
-RES_BUFS = FIRST_AHEAD + LAST_BEHIND + 1
+RES_BUFS = FIRST_AHEAD + LAST_BEHIND - 1
 
 FLOPS = 4 * 2 * C * C * N + 2 * 2 * P * P * P * CB * NBLK
 
@@ -36,9 +36,11 @@ def tile_proteintransformer_b_kernel(
         tc.tile_pool(name="held", bufs=1) as held,
         tc.tile_pool(name="posp", bufs=POS_AHEAD + 1) as posp,
         tc.tile_pool(name="resp", bufs=RES_BUFS) as resp,
-        tc.tile_pool(name="blockp", bufs=3) as blockp,
-        tc.tile_pool(name="valuep", bufs=5) as valuep,
-        tc.tile_pool(name="ctxp", bufs=HELD_BACK + 2) as ctxp,
+        tc.tile_pool(name="blockp", bufs=2) as blockp,
+        tc.tile_pool(name="embp", bufs=1) as embp,
+        tc.tile_pool(name="smallp", bufs=3) as smallp,
+        tc.tile_pool(name="valuep", bufs=4) as valuep,
+        tc.tile_pool(name="ctxp", bufs=HELD_BACK + 1) as ctxp,
         tc.psum_pool(name="one_ps", bufs=1) as one_ps,
         tc.psum_pool(name="two_ps", bufs=2) as two_ps,
         tc.psum_pool(name="wide_ps", bufs=3) as wide_ps,
@@ -94,13 +96,13 @@ def tile_proteintransformer_b_kernel(
         nc.vector.memset(minus_half[:], -0.5)
 
         def moments(j, z, norm):
-            stats = blockp.tile([P, 6], F32, name="stats" + norm)
+            stats = smallp.tile([P, 6], F32, name="stats" + norm)
             nc.vector.bn_stats(stats[:], z)
-            mean_var = blockp.tile([P, 2], F32, name="mean_var" + norm)
+            mean_var = smallp.tile([P, 2], F32, name="mean_var" + norm)
             nc.vector.bn_aggr(mean_var[:], stats[:])
-            var_eps = blockp.tile([P, 1], F32, name="var_eps" + norm)
+            var_eps = smallp.tile([P, 1], F32, name="var_eps" + norm)
             nc.vector.tensor_scalar_add(var_eps[:], mean_var[:, 1:2], EPS)
-            rstd = blockp.tile([P, 1], F32, name="rstd" + norm)
+            rstd = smallp.tile([P, 1], F32, name="rstd" + norm)
             nc.gpsimd.tensor_tensor(rstd[:], var_eps[:], minus_half[:], ALU.pow)
             tile_of["mean_var" + norm, j] = mean_var
             tile_of["rstd" + norm, j] = rstd
@@ -112,7 +114,7 @@ def tile_proteintransformer_b_kernel(
             return back_ps
 
         def look_up(j):
-            emb = blockp.tile([P, CB, P], F32, name="emb")
+            emb = embp.tile([P, CB, P], F32, name="emb")
             piece = offsets[:, j * (P // 16) : (j + 1) * (P // 16)]
             for b in range(CB):
                 nc.vector.tensor_tensor(emb[:, b, :], tok[b][:].indirect(piece), tile_of["pos", j][:, b, :], ALU.add)
@@ -192,13 +194,13 @@ def tile_proteintransformer_b_kernel(
             tile_of["s_ps", j] = s_ps
 
         def row_max(j):
-            neg_top = blockp.tile([P, CB], F32, name="neg_top")
+            neg_top = smallp.tile([P, CB], F32, name="neg_top")
             nc.vector.reduce_max(neg_top[:], tile_of["s_ps", j][:], axis=AX.X, negate=True)
             tile_of["neg_top", j] = neg_top
 
         def exponentials(j):
             expo = blockp.tile([P, CB, P], F32, name="expo")
-            total = blockp.tile([P, CB], F32, name="total")
+            total = smallp.tile([P, CB], F32, name="total")
             for h in range(CB):
                 nc.scalar.activation(
                     expo[:, h, :], tile_of["s_ps", j][:, h, :], ACT.Exp,
@@ -208,7 +210,7 @@ def tile_proteintransformer_b_kernel(
             tile_of["total", j] = total
 
         def invert_sums(j):
-            inv = blockp.tile([P, CB], F32, name="inv")
+            inv = smallp.tile([P, CB], F32, name="inv")
             nc.vector.reciprocal(inv[:], tile_of["total", j][:])
             tile_of["inv", j] = inv
 

@@ -38,6 +38,7 @@ def tile_proteintransformer_b_kernel(
         tc.tile_pool(name="resp", bufs=RES_BUFS) as resp,
         tc.tile_pool(name="blockp", bufs=2) as blockp,
         tc.tile_pool(name="embp", bufs=1) as embp,
+        tc.tile_pool(name="znp", bufs=1) as znp,
         tc.tile_pool(name="smallp", bufs=3) as smallp,
         tc.tile_pool(name="valuep", bufs=4) as valuep,
         tc.tile_pool(name="ctxp", bufs=HELD_BACK + 1) as ctxp,
@@ -259,7 +260,7 @@ def tile_proteintransformer_b_kernel(
             moments(j, tile_of["res", j][:], "_y")
 
         def normalise_y(j):
-            zn = blockp.tile([P, C], F32, name="zn")
+            zn = znp.tile([P, C], F32, name="zn")
             nc.vector.tensor_scalar(
                 zn[:], tile_of["res", j][:], tile_of["mean_var_y", j][:, 0:1], tile_of["rstd_y", j][:], ALU.subtract, ALU.mult
             )
@@ -299,9 +300,9 @@ def tile_proteintransformer_b_kernel(
             at(project_v, s)
             at(copy_context, s - 3)
             at(weights, s - 2)
+            at(flip_out, s - 6 - HELD_BACK)
             at(normalise_y, s - 5 - HELD_BACK)
             at(look_up, s + 4)
-            at(flip_out, s - 6 - HELD_BACK)
             at(round_k, s)
             at(project_out, s - 3 - HELD_BACK)
             at(round_x, s + 1)

@@ -21,7 +21,7 @@ EPS = 1e-5
 SCALE = 1.0 / math.sqrt(P)
 
 FIRST_AHEAD = 4
-HELD_BACK = 2
+HELD_BACK = 1
 LAST_BEHIND = 6 + HELD_BACK
 RES_BUFS = FIRST_AHEAD + LAST_BEHIND - 1
 

import math

import concourse.mybir as mybir
from concourse.masks import make_identity

F32 = mybir.dt.float32
BF16 = mybir.dt.bfloat16
U16 = mybir.dt.uint16
ALU = mybir.AluOpType
ACT = mybir.ActivationFunctionType
AX = mybir.AxisListType

P = 128
C = 512
VOCAB = 4096
N = 2048
CB = C // P
NBLK = N // P
POS_AHEAD = 4
EPS = 1e-5
SCALE = 1.0 / math.sqrt(P)

FIRST_AHEAD = 4
HELD_BACK = 1
LAST_BEHIND = 6 + HELD_BACK
RES_BUFS = FIRST_AHEAD + LAST_BEHIND - 1

FLOPS = 4 * 2 * C * C * N + 2 * 2 * P * P * P * CB * NBLK


def tile_proteintransformer_b_kernel(
    tc, tok_emb, pos_emb, gain_e, bias_e, wq, wk, wv, wo, gain1, bias1, offs, out
):
    nc = tc.nc
    with (
        tc.tile_pool(name="held", bufs=1) as held,
        tc.tile_pool(name="posp", bufs=POS_AHEAD + 1) as posp,
        tc.tile_pool(name="resp", bufs=RES_BUFS) as resp,
        tc.tile_pool(name="blockp", bufs=2) as blockp,
        tc.tile_pool(name="embp", bufs=1) as embp,
        tc.tile_pool(name="znp", bufs=1) as znp,
        tc.tile_pool(name="smallp", bufs=3) as smallp,
        tc.tile_pool(name="valuep", bufs=4) as valuep,
        tc.tile_pool(name="ctxp", bufs=HELD_BACK + 1) as ctxp,
        tc.psum_pool(name="one_ps", bufs=1) as one_ps,
        tc.psum_pool(name="two_ps", bufs=2) as two_ps,
        tc.psum_pool(name="wide_ps", bufs=3) as wide_ps,
    ):
        tile_of = {}

        offsets = held.tile([P, N // 16], U16, name="offsets")
        nc.sync.dma_start(offsets[:], offs)

        pos_view = pos_emb.rearrange("(b p) n -> p b n", p=P)
        out_view = out.rearrange("(b p) n -> p b n", p=P)

        def load_pos(j):
            pos = posp.tile([P, CB, P], F32, name="pos")
            nc.sync.dma_start(pos[:], pos_view[:, :, j * P : (j + 1) * P])
            tile_of["pos", j] = pos

        def load_row(vec, name):
            row = held.tile([P, C], F32, name=name)
            nc.sync.dma_start(row[:], vec.rearrange("c o -> (o c)").partition_broadcast(P))
            return row

        def load_weight(w, name):
            w_sb = held.tile([P, CB, C], BF16, name=name)
            nc.sync.dma_start(w_sb[:], w.rearrange("(kb p) m -> p kb m", p=P))
            return w_sb

        load_pos(0)
        tok = [held.tile([P, VOCAB], F32, name="tok%d" % b) for b in range(CB)]
        for b in range(CB):
            nc.sync.dma_start(tok[b][:], tok_emb[b * P : (b + 1) * P, :])
        gain_row = load_row(gain_e, "gain_row")
        load_pos(1)
        bias_row = load_row(bias_e, "bias_row")
        wq_sb = load_weight(wq, "wq_sb")
        load_pos(2)
        wk_sb = load_weight(wk, "wk_sb")
        wv_sb = load_weight(wv, "wv_sb")
        load_pos(3)
        wo_sb = load_weight(wo, "wo_sb")

        gain1_sb = held.tile([P, CB], F32, name="gain1_sb")
        bias1_sb = held.tile([P, CB], F32, name="bias1_sb")
        with nc.allow_non_contiguous_dma(reason="four values to a partition"):
            nc.scalar.dma_start(gain1_sb[:], gain1.rearrange("(b p) o -> p (b o)", p=P))
            nc.scalar.dma_start(bias1_sb[:], bias1.rearrange("(b p) o -> p (b o)", p=P))

        ident_f32 = held.tile([P, P], F32, name="ident_f32")
        make_identity(nc, ident_f32[:])
        ident_bf = held.tile([P, P], BF16, name="ident_bf")
        make_identity(nc, ident_bf[:])
        minus_half = held.tile([P, 1], F32, name="minus_half")
        nc.vector.memset(minus_half[:], -0.5)

        def moments(j, z, norm):
            stats = smallp.tile([P, 6], F32, name="stats" + norm)
            nc.vector.bn_stats(stats[:], z)
            mean_var = smallp.tile([P, 2], F32, name="mean_var" + norm)
            nc.vector.bn_aggr(mean_var[:], stats[:])
            var_eps = smallp.tile([P, 1], F32, name="var_eps" + norm)
            nc.vector.tensor_scalar_add(var_eps[:], mean_var[:, 1:2], EPS)
            rstd = smallp.tile([P, 1], F32, name="rstd" + norm)
            nc.gpsimd.tensor_tensor(rstd[:], var_eps[:], minus_half[:], ALU.pow)
            tile_of["mean_var" + norm, j] = mean_var
            tile_of["rstd" + norm, j] = rstd

        def flip_back(z, pool, tag):
            back_ps = pool.tile([P, CB, P], F32, name="back_ps", tag=tag)
            for b in range(CB):
                nc.tensor.transpose(back_ps[:, b, :], z[:, b * P : (b + 1) * P], ident_f32[:])
            return back_ps

        def look_up(j):
            emb = embp.tile([P, CB, P], F32, name="emb")
            piece = offsets[:, j * (P // 16) : (j + 1) * (P // 16)]
            for b in range(CB):
                nc.vector.tensor_tensor(emb[:, b, :], tok[b][:].indirect(piece), tile_of["pos", j][:, b, :], ALU.add)
            if j + POS_AHEAD < NBLK:
                load_pos(j + POS_AHEAD)
            tile_of["emb", j] = emb

        def flip_e(j):
            eT_ps = two_ps.tile([P, C], F32, name="eT_ps", tag="e_or_s")
            for b in range(CB):
                nc.tensor.transpose(eT_ps[:, b * P : (b + 1) * P], tile_of["emb", j][:, b, :], ident_f32[:])
            tile_of["eT_ps", j] = eT_ps

        def centre_e(j):
            eT_ps = tile_of["eT_ps", j]
            moments(j, eT_ps[:], "_e")
            res = resp.tile([P, C], F32, name="res")
            nc.vector.scalar_tensor_tensor(
                res[:], eT_ps[:], tile_of["mean_var_e", j][:, 0:1], gain_row[:], ALU.subtract, ALU.mult
            )
            tile_of["res", j] = res

        def finish_x(j):
            res = tile_of["res", j]
            nc.vector.scalar_tensor_tensor(res[:], res[:], tile_of["rstd_e", j][:], bias_row[:], ALU.mult, ALU.add)

        def flip_x(j):
            tile_of["x_ps", j] = flip_back(tile_of["res", j], two_ps, "x_or_w")

        def round_x(j):
            x_bf = blockp.tile([P, CB, P], BF16, name="x_bf")
            nc.scalar.copy(x_bf[:], tile_of["x_ps", j][:])
            tile_of["x_bf", j] = x_bf

        def project_heads(j, w_sb, name):
            x_bf = tile_of["x_bf", j]
            acc = wide_ps.tile([P, C], F32, name="acc")
            for h in range(CB):
                head = slice(h * P, (h + 1) * P)
                for kb in range(CB):
                    nc.tensor.matmul(acc[:, head], w_sb[:, kb, head], x_bf[:, kb, :], start=(kb == 0), stop=(kb == CB - 1))
            tile_of[name + "_ps", j] = acc

        def project_q(j):
            project_heads(j, wq_sb, "q")

        def project_k(j):
            project_heads(j, wk_sb, "k")

        def project_v(j):
            x_bf = tile_of["x_bf", j]
            acc = wide_ps.tile([P, C], F32, name="acc")
            for kb in range(CB):
                nc.tensor.matmul(acc[:], x_bf[:, kb, :], wv_sb[:, kb, :], start=(kb == 0), stop=(kb == CB - 1))
            tile_of["v_ps", j] = acc

        def round_q(j):
            q_bf = blockp.tile([P, C], BF16, name="q_bf")
            nc.scalar.mul(q_bf[:], tile_of["q_ps", j][:], SCALE)
            tile_of["q_bf", j] = q_bf

        def round_k(j):
            k_bf = blockp.tile([P, C], BF16, name="k_bf")
            nc.scalar.copy(k_bf[:], tile_of["k_ps", j][:])
            tile_of["k_bf", j] = k_bf

        def round_v(j):
            v_bf = valuep.tile([P, C], BF16, name="v_bf")
            nc.scalar.copy(v_bf[:], tile_of["v_ps", j][:])
            tile_of["v_bf", j] = v_bf

        def scores(j):
            s_ps = two_ps.tile([P, CB, P], F32, name="s_ps", tag="e_or_s")
            for h in range(CB):
                head = slice(h * P, (h + 1) * P)
                nc.tensor.matmul(s_ps[:, h, :], tile_of["q_bf", j][:, head], tile_of["k_bf", j][:, head], start=True, stop=True)
            tile_of["s_ps", j] = s_ps

        def row_max(j):
            neg_top = smallp.tile([P, CB], F32, name="neg_top")
            nc.vector.reduce_max(neg_top[:], tile_of["s_ps", j][:], axis=AX.X, negate=True)
            tile_of["neg_top", j] = neg_top

        def exponentials(j):
            expo = blockp.tile([P, CB, P], F32, name="expo")
            total = smallp.tile([P, CB], F32, name="total")
            for h in range(CB):
                nc.scalar.activation(
                    expo[:, h, :], tile_of["s_ps", j][:, h, :], ACT.Exp,
                    bias=tile_of["neg_top", j][:, h : h + 1], accum_out=total[:, h : h + 1],
                )
            tile_of["expo", j] = expo
            tile_of["total", j] = total

        def invert_sums(j):
            inv = smallp.tile([P, CB], F32, name="inv")
            nc.vector.reciprocal(inv[:], tile_of["total", j][:])
            tile_of["inv", j] = inv

        def weights(j):
            a_bf = blockp.tile([P, CB, P], BF16, name="a_bf")
            for h in range(CB):
                nc.scalar.activation(
                    a_bf[:, h, :], tile_of["expo", j][:, h, :], ACT.Copy, scale=tile_of["inv", j][:, h : h + 1]
                )
            tile_of["a_bf", j] = a_bf

        def flip_weights(j):
            flip_ctx = two_ps.tile([P, 2, CB, P], BF16, name="flip_ctx", tag="x_or_w")
            for h in range(CB):
                nc.tensor.transpose(flip_ctx[:, 0, h, :], tile_of["a_bf", j][:, h, :], ident_bf[:])
            tile_of["flip_ctx", j] = flip_ctx

        def copy_weights(j):
            aT_bf = blockp.tile([P, CB, P], BF16, name="aT_bf")
            nc.scalar.copy(aT_bf[:], tile_of["flip_ctx", j][:, 0, :, :])
            tile_of["aT_bf", j] = aT_bf

        def context(j):
            for h in range(CB):
                nc.tensor.matmul(
                    tile_of["flip_ctx", j][:, 1, h, :], tile_of["v_bf", j][:, h * P : (h + 1) * P], tile_of["aT_bf", j][:, h, :],
                    start=True, stop=True,
                )

        def copy_context(j):
            ctx_bf = ctxp.tile([P, CB, P], BF16, name="ctx_bf")
            nc.vector.tensor_copy(ctx_bf[:], tile_of["flip_ctx", j][:, 1, :, :])
            tile_of["ctx_bf", j] = ctx_bf

        def project_out(j):
            yT_ps = wide_ps.tile([P, C], F32, name="yT_ps", tag="acc")
            for kb in range(CB):
                nc.tensor.matmul(yT_ps[:], tile_of["ctx_bf", j][:, kb, :], wo_sb[:, kb, :], start=(kb == 0), stop=(kb == CB - 1))
            tile_of["yT_ps", j] = yT_ps

        def add_residual(j):
            res = tile_of["res", j]
            nc.vector.tensor_tensor(res[:], tile_of["yT_ps", j][:], res[:], ALU.add)

        def moments_y(j):
            moments(j, tile_of["res", j][:], "_y")

        def normalise_y(j):
            zn = znp.tile([P, C], F32, name="zn")
            nc.vector.tensor_scalar(
                zn[:], tile_of["res", j][:], tile_of["mean_var_y", j][:, 0:1], tile_of["rstd_y", j][:], ALU.subtract, ALU.mult
            )
            tile_of["zn", j] = zn

        def flip_out(j):
            tile_of["zn_ps", j] = flip_back(tile_of["zn", j], one_ps, "out_ps")

        def store(j):
            done = blockp.tile([P, CB, P], F32, name="done")
            for b in range(CB):
                nc.scalar.activation(
                    done[:, b, :], tile_of["zn_ps", j][:, b, :], ACT.Identity,
                    bias=bias1_sb[:, b : b + 1], scale=gain1_sb[:, b : b + 1],
                )
            nc.sync.dma_start(out_view[:, :, j * P : (j + 1) * P], done[:])

        def at(piece, j):
            if 0 <= j < NBLK:
                piece(j)

        for s in range(-FIRST_AHEAD, NBLK + LAST_BEHIND):
            at(flip_e, s + 3)
            at(project_q, s)
            at(add_residual, s - 4 - HELD_BACK)
            at(copy_weights, s - 3)
            at(moments_y, s - 4 - HELD_BACK)
            at(project_k, s)
            at(centre_e, s + 3)
            at(row_max, s - 2)
            at(exponentials, s - 2)
            at(round_q, s)
            at(context, s - 3)
            at(finish_x, s + 1)
            at(invert_sums, s - 2)
            at(flip_x, s + 1)
            at(project_v, s)
            at(copy_context, s - 3)
            at(weights, s - 2)
            at(flip_out, s - 6 - HELD_BACK)
            at(normalise_y, s - 5 - HELD_BACK)
            at(look_up, s + 4)
            at(round_k, s)
            at(project_out, s - 3 - HELD_BACK)
            at(round_x, s + 1)
            at(round_v, s)
            at(scores, s - 1)
            at(flip_weights, s - 2)
            at(store, s - 6 - HELD_BACK)
